import numpy as np
import ml_dtypes


def mxq(x, axis, fmt="e4m3"):
    dtype, down = {"e4m3": (ml_dtypes.float8_e4m3fn, 7), "e5m2": (ml_dtypes.float8_e5m2, 14)}[fmt]
    v = np.moveaxis(np.asarray(x, np.float32).astype(ml_dtypes.bfloat16).astype(np.float64), axis, -1)
    blocks = v.reshape(v.shape[:-1] + (-1, 32))
    amax = np.abs(blocks).max(-1, keepdims=True)
    byte = np.maximum(np.where(amax > 0, np.frexp(amax)[1] - 1 + 127, 0) - down, 1)
    scale = np.exp2(byte - 127.0)
    codes = (blocks / scale).astype(np.float32).astype(dtype).astype(np.float64)
    return np.moveaxis((codes * scale).reshape(v.shape), -1, axis)


WIDE = False


def mx_kscale(k):
    if not WIDE:
        return np.ones(k)
    levels = np.array([10, -10, 5, -5, 0])
    a = np.random.permutation(np.resize(levels, k // 512 * 4)).reshape(k // 512, 4)
    idx = np.arange(k)
    return np.exp2(a[idx // 512, idx % 128 // 32])


BF16 = ml_dtypes.bfloat16


def bf(x):
    return np.asarray(x, np.float32).astype(BF16)


def f64(x):
    return np.asarray(x).astype(np.float64)


N, D_IN, D_HID, D_OUT = 2048, 512, 256, 256
NEG = -3.4028234663852886e38
QS = np.sqrt(2.0) / D_HID ** 0.25


def setup_inputs():
    s = mx_kscale(D_IN)
    A = np.random.randint(0, 2, (N, N), dtype=np.int32)
    A = A * (1 - np.eye(N, dtype=np.int32))
    return {"X": bf(np.random.standard_normal((N, D_IN)) * s),
            "A": A,
            "Q": bf(np.random.standard_normal((N, D_HID)) * QS),
            "K": bf(np.random.standard_normal((N, D_HID)) * QS),
            "Wv": bf(np.random.standard_normal((D_IN, D_OUT)) / np.sqrt(D_IN) / s[:, None])}


def reference(X, A, Q, K, Wv):
    Af = f64(A) + np.eye(N)
    V = mxq(f64(X), 1, "e4m3") @ mxq(f64(Wv), 0, "e4m3")
    S = f64(Q) @ f64(K).T
    Z = S + NEG * (1.0 - Af)
    e = np.exp(Z - Z.max(1, keepdims=True))
    return (mxq(e, 1, "e4m3") @ mxq(V, 0, "e4m3")) / e.sum(1, keepdims=True)

@@ -1,0 +1,293 @@
+from contextlib import ExitStack
+
+import concourse.mybir as mybir
+from concourse.masks import make_identity
+
+F32 = mybir.dt.float32
+BF16 = mybir.dt.bfloat16
+I32 = mybir.dt.int32
+U32 = mybir.dt.uint32
+U8 = mybir.dt.uint8
+FP8X4 = mybir.dt.float8_e4m3fn_x4
+ALU = mybir.AluOpType
+ACT = mybir.ActivationFunctionType
+AXIS_X = mybir.AxisListType.X
+
+P = 128
+PACK = 4
+K_PASS = P * PACK
+BANK = 512
+
+N_NODES = 2048
+D_IN = 512
+D_HID = 256
+D_OUT = 256
+
+N_BLOCKS = N_NODES // P
+N_PASSES = N_NODES // K_PASS
+N_CHUNKS = N_NODES // BANK
+H_HALVES = D_HID // P
+
+NO_EDGE = -(2.0**126)
+
+VECTOR_COLS = 1024
+
+FLOPS = 2 * N_NODES * (D_IN * D_OUT + N_NODES * D_HID + N_NODES * D_OUT)
+
+
+def tile_gatconv_pa_kernel(tc, X, A, Q, K, Wv, out):
+    nc = tc.nc
+    with ExitStack() as stack:
+        keep = stack.enter_context(tc.tile_pool(name="keep", bufs=1))
+        stage = stack.enter_context(tc.tile_pool(name="stage", bufs=3))
+        stats = stack.enter_context(tc.tile_pool(name="stats", bufs=4))
+        adjacency = stack.enter_context(tc.tile_pool(name="adjacency", bufs=3))
+        psum_s = stack.enter_context(tc.psum_pool(name="psum_s", bufs=4))
+        psum_t = stack.enter_context(tc.psum_pool(name="psum_t", bufs=2))
+        psum_o = stack.enter_context(tc.psum_pool(name="psum_o", bufs=2))
+
+        def copy_out(piece, dst, src):
+            if piece % 2 == 0:
+                nc.scalar.copy(out=dst, in_=src)
+            else:
+                nc.vector.tensor_copy(out=dst, in_=src)
+
+        k_raw = keep.tile([P, N_BLOCKS, D_HID], BF16)
+        q_raw = keep.tile([P, N_BLOCKS, D_HID], BF16)
+        x_raw = keep.tile([P, N_BLOCKS, D_IN], BF16)
+        k_view = K.rearrange("(t p) h -> p t h", p=P)
+        q_view = Q.rearrange("(t p) h -> p t h", p=P)
+        x_view = X.rearrange("(t p) f -> p t f", p=P)
+        for t0 in range(0, N_BLOCKS, 4):
+            nc.sync.dma_start(out=k_raw[:, t0 : t0 + 4, :], in_=k_view[:, t0 : t0 + 4, :])
+        for t0 in range(0, N_BLOCKS, 4):
+            nc.sync.dma_start(out=q_raw[:, t0 : t0 + 4, :], in_=q_view[:, t0 : t0 + 4, :])
+        wv_raw = keep.tile([P, PACK, D_OUT], BF16)
+        nc.sync.dma_start(
+            out=wv_raw[:].rearrange("p (u e) n -> p u (e n)", u=2),
+            in_=Wv.rearrange("(u p e) n -> p u (e n)", u=2, p=P, e=2),
+        )
+        for t0 in range(0, N_BLOCKS, 4):
+            nc.sync.dma_start(out=x_raw[:, t0 : t0 + 4, :], in_=x_view[:, t0 : t0 + 4, :])
+
+        block = {b: {} for b in range(N_BLOCKS)}
+
+        def load_adjacency(b):
+            a_blk = adjacency.tile([P, N_NODES, 2], I32)
+            nc.sync.dma_start(
+                out=a_blk[:].rearrange("p j w -> p (j w)"), in_=A.bitcast(I32)[b * P : (b + 1) * P, :]
+            )
+            block[b]["edges"] = a_blk[:, :, 0]
+            block[b]["edges_u32"] = a_blk[:].bitcast(U32)[:, :, 0]
+
+        for b in range(3):
+            load_adjacency(b)
+
+        ident_bf = keep.tile([P, P], BF16)
+        make_identity(nc, ident_bf[:])
+        ident_f32 = keep.tile([P, P], F32)
+        make_identity(nc, ident_f32[:])
+        off_diagonal = keep.tile([P, P], BF16)
+        nc.vector.tensor_scalar(
+            out=off_diagonal[:], in0=ident_bf[:], scalar1=-1.0, scalar2=1.0, op0=ALU.mult, op1=ALU.add
+        )
+
+        kT = keep.tile([P, H_HALVES, N_NODES], BF16)
+        qT = keep.tile([P, H_HALVES, N_NODES], BF16)
+        for raw, flipped in ((k_raw, kT), (q_raw, qT)):
+            for t0 in range(0, N_BLOCKS, 4):
+                flip_ps = psum_t.tile([P, H_HALVES, 4, P], BF16, tag="t")
+                for half in range(H_HALVES):
+                    for a in range(4):
+                        nc.tensor.transpose(
+                            flip_ps[:, half, a, :], raw[:, t0 + a, half * P : (half + 1) * P], ident_bf[:]
+                        )
+                copy_out(
+                    t0 // 4,
+                    flipped[:, :, t0 * P : (t0 + 4) * P],
+                    flip_ps[:].rearrange("p h a j -> p h (a j)"),
+                )
+
+        wv_grouped = keep.tile([P, D_OUT, PACK], BF16, align_bytes=64)
+        nc.vector.tensor_copy(out=wv_grouped[:], in_=wv_raw[:].rearrange("p t n -> p n t"))
+        wv_codes = keep.tile([P, D_OUT], U32, align_bytes=64)
+        wv_scales = keep.tile([P, D_OUT], U8, align_bytes=64)
+
+        x_words = x_raw[:].bitcast(F32)
+        x_grouped = keep.tile([P, N_BLOCKS, P, PACK], BF16, align_bytes=64)
+        x_grouped_words = x_grouped[:].bitcast(F32)
+        x_codes = keep.tile([P, N_BLOCKS, P], U32, align_bytes=64)
+        x_scales = keep.tile([P, N_BLOCKS, P], U8, align_bytes=64)
+        v_grouped = keep.tile([P, N_PASSES, D_OUT, PACK], BF16, align_bytes=64)
+        v_codes = keep.tile([P, N_PASSES, D_OUT], U32, align_bytes=64)
+        v_scales = keep.tile([P, N_PASSES, D_OUT], U8, align_bytes=64)
+        for t0 in range(0, N_BLOCKS, 2):
+            xt_ps = psum_t.tile([P, 2, 2, P], F32, tag="t")
+            for a in range(2):
+                for u in range(2):
+                    nc.tensor.transpose(xt_ps[:, a, u, :], x_words[:, t0 + a, u * P : (u + 1) * P], ident_f32[:])
+            copy_out(t0 // 2, x_grouped_words[:, t0 : t0 + 2, :, :], xt_ps[:].rearrange("p a u r -> p a r u"))
+        nc.vector.quantize_mx(
+            out=wv_codes[:].bitcast(FP8X4),
+            scales=wv_scales[:],
+            in_=wv_grouped[:].rearrange("p n t -> p (n t)"),
+        )
+        for g in range(N_PASSES):
+            tiles = slice(g * PACK, (g + 1) * PACK)
+            nc.vector.quantize_mx(
+                out=x_codes[:, tiles, :].rearrange("p t r -> p (t r)").bitcast(FP8X4),
+                scales=x_scales[:, tiles, :].rearrange("p t r -> p (t r)"),
+                in_=x_grouped[:, tiles, :, :].rearrange("p t r k -> p (t r k)"),
+            )
+        for g in range(N_PASSES):
+            for half in range(D_OUT // P):
+                cols = slice(half * P, (half + 1) * P)
+                v_ps = psum_s.tile([P, PACK, P], F32, tag="s")
+                for t in range(PACK):
+                    nc.tensor.matmul_mx(
+                        out=v_ps[:, t, :],
+                        lhsT=x_codes[:, g * PACK + t, :].bitcast(FP8X4),
+                        lhsT_scale=x_scales[:, g * PACK + t, :],
+                        rhs=wv_codes[:, cols].bitcast(FP8X4),
+                        rhs_scale=wv_scales[:, cols],
+                        start=True,
+                        stop=True,
+                    )
+                copy_out(half, v_grouped[:, g, cols, :], v_ps[:].rearrange("p t d -> p d t"))
+        for g in range(N_PASSES):
+            nc.vector.quantize_mx(
+                out=v_codes[:, g, :].bitcast(FP8X4),
+                scales=v_scales[:, g, :],
+                in_=v_grouped[:, g, :, :].rearrange("p d t -> p (d t)"),
+            )
+
+        def mask_on_scalar(b):
+            mask = stage.tile([P, N_NODES], BF16)
+            block[b]["mask"] = mask
+            nc.scalar.activation(
+                out=mask[:, VECTOR_COLS:],
+                in_=block[b]["edges_u32"][:, VECTOR_COLS:],
+                func=ACT.Copy,
+                scale=-NO_EDGE,
+                bias=NO_EDGE,
+            )
+
+        def mask_on_vector(b):
+            mask = block[b]["mask"]
+            nc.vector.tensor_scalar(
+                out=mask[:, :VECTOR_COLS],
+                in0=block[b]["edges"][:, :VECTOR_COLS],
+                scalar1=1.0,
+                scalar2=-NO_EDGE,
+                op0=ALU.subtract,
+                op1=ALU.mult,
+            )
+            own = mask[:, b * P : (b + 1) * P]
+            nc.vector.tensor_tensor(out=own, in0=own, in1=off_diagonal[:], op=ALU.mult)
+
+        def score_matmuls(b):
+            rows = slice(b * P, (b + 1) * P)
+            block[b]["s"] = []
+            for c in range(N_CHUNKS):
+                s_ps = psum_s.tile([P, BANK], F32, tag="s")
+                for half in range(H_HALVES):
+                    nc.tensor.matmul(
+                        out=s_ps[:],
+                        lhsT=qT[:, half, rows],
+                        rhs=kT[:, half, c * BANK : (c + 1) * BANK],
+                        start=(half == 0),
+                        stop=(half == H_HALVES - 1),
+                    )
+                block[b]["s"].append(s_ps)
+
+        def masked_scores(b):
+            z = stage.tile([P, N_NODES], F32)
+            for c in range(N_CHUNKS):
+                cols = slice(c * BANK, (c + 1) * BANK)
+                nc.vector.tensor_tensor(
+                    out=z[:, cols], in0=block[b]["s"][c][:], in1=block[b]["mask"][:, cols], op=ALU.add
+                )
+            neg_max = stats.tile([P, 1], F32)
+            nc.vector.tensor_reduce(out=neg_max[:], in_=z[:], axis=AXIS_X, op=ALU.max, negate=True)
+            block[b]["z"] = z
+            block[b]["neg_max"] = neg_max
+
+        def exponentials(b):
+            e_blk = stage.tile([P, N_NODES], BF16)
+            row_sum = stats.tile([P, 1], F32)
+            nc.scalar.activation(
+                out=e_blk[:],
+                in_=block[b]["z"][:],
+                func=ACT.Exp,
+                bias=block[b]["neg_max"][:],
+                scale=1.0,
+                accum_out=row_sum[:],
+            )
+            block[b]["e"] = e_blk
+            block[b]["row_sum"] = row_sum
+
+        def transposes(b):
+            block[b]["eT"] = []
+            for g0 in range(0, N_PASSES, 2):
+                et_ps = psum_t.tile([P, 2, PACK, P], BF16, tag="t")
+                for a in range(2):
+                    for t in range(PACK):
+                        j0 = (g0 + a) * K_PASS + t * P
+                        nc.tensor.transpose(et_ps[:, a, t, :], block[b]["e"][:, j0 : j0 + P], ident_bf[:])
+                block[b]["eT"].append(et_ps)
+
+        def regroup(b):
+            e_grouped = stage.tile([P, N_PASSES, P, PACK], BF16, align_bytes=64)
+            for g0 in range(0, N_PASSES, 2):
+                nc.scalar.copy(
+                    out=e_grouped[:, g0 : g0 + 2, :, :],
+                    in_=block[b]["eT"][g0 // 2][:].rearrange("p a t i -> p a i t"),
+                )
+            block[b]["e_grouped"] = e_grouped
+
+        def quantise(b):
+            e_codes = stage.tile([P, N_PASSES, P], U32, align_bytes=64)
+            e_scales = stage.tile([P, N_PASSES, P], U8, align_bytes=64)
+            nc.vector.quantize_mx(
+                out=e_codes[:].rearrange("p g i -> p (g i)").bitcast(FP8X4),
+                scales=e_scales[:].rearrange("p g i -> p (g i)"),
+                in_=block[b]["e_grouped"][:].rearrange("p g i t -> p (g i t)"),
+            )
+            block[b]["e_codes"] = e_codes
+            block[b]["e_scales"] = e_scales
+            inv_sum = stats.tile([P, 1], F32)
+            nc.vector.reciprocal(out=inv_sum[:], in_=block[b]["row_sum"][:])
+            block[b]["inv_sum"] = inv_sum
+
+        def weighted_sum(b):
+            o_ps = psum_o.tile([P, D_OUT], F32)
+            for g in range(N_PASSES):
+                nc.tensor.matmul_mx(
+                    out=o_ps[:],
+                    lhsT=block[b]["e_codes"][:, g, :].bitcast(FP8X4),
+                    lhsT_scale=block[b]["e_scales"][:, g, :],
+                    rhs=v_codes[:, g, :].bitcast(FP8X4),
+                    rhs_scale=v_scales[:, g, :],
+                    start=(g == 0),
+                    stop=(g == N_PASSES - 1),
+                )
+            block[b]["o"] = o_ps
+
+        def finish(b):
+            o_sb = stage.tile([P, D_OUT], F32)
+            nc.scalar.activation(out=o_sb[:], in_=block[b]["o"][:], func=ACT.Copy, scale=block[b]["inv_sum"][:])
+            nc.gpsimd.dma_start(out=out[b * P : (b + 1) * P, :], in_=o_sb[:])
+
+        for b in range(N_BLOCKS):
+            if b + 3 < N_BLOCKS:
+                load_adjacency(b + 3)
+            mask_on_scalar(b)
+            mask_on_vector(b)
+            score_matmuls(b)
+            masked_scores(b)
+            exponentials(b)
+            transposes(b)
+            regroup(b)
+            quantise(b)
+            weighted_sum(b)
+            finish(b)

@@ -28,9 +28,11 @@ N_PASSES = N_NODES // K_PASS
 N_CHUNKS = N_NODES // BANK
 H_HALVES = D_HID // P
 
-NO_EDGE = -(2.0**126)
+NO_EDGE = 2.0**126
 
-VECTOR_COLS = 1024
+SELF_SCORE = 48.0
+
+AHEAD = 4
 
 FLOPS = 2 * N_NODES * (D_IN * D_OUT + N_NODES * D_HID + N_NODES * D_OUT)
 
@@ -40,11 +42,12 @@ def tile_gatconv_pa_kernel(tc, X, A, Q, K, Wv, out):
     with ExitStack() as stack:
         keep = stack.enter_context(tc.tile_pool(name="keep", bufs=1))
         stage = stack.enter_context(tc.tile_pool(name="stage", bufs=3))
+        zs = stack.enter_context(tc.tile_pool(name="zs", bufs=3))
         stats = stack.enter_context(tc.tile_pool(name="stats", bufs=4))
-        adjacency = stack.enter_context(tc.tile_pool(name="adjacency", bufs=3))
+        adjacency = stack.enter_context(tc.tile_pool(name="adjacency", bufs=4))
         psum_s = stack.enter_context(tc.psum_pool(name="psum_s", bufs=4))
-        psum_t = stack.enter_context(tc.psum_pool(name="psum_t", bufs=2))
-        psum_o = stack.enter_context(tc.psum_pool(name="psum_o", bufs=2))
+        psum_t = stack.enter_context(tc.psum_pool(name="psum_t", bufs=3))
+        psum_o = stack.enter_context(tc.psum_pool(name="psum_o", bufs=1))
 
         def copy_out(piece, dst, src):
             if piece % 2 == 0:
@@ -57,7 +60,7 @@ def tile_gatconv_pa_kernel(tc, X, A, Q, K, Wv, out):
         x_raw = keep.tile([P, N_BLOCKS, D_IN], BF16)
         k_view = K.rearrange("(t p) h -> p t h", p=P)
         q_view = Q.rearrange("(t p) h -> p t h", p=P)
-        x_view = X.rearrange("(t p) f -> p t f", p=P)
+        x_view = X.rearrange("(v p r) f -> p v (r f)", p=P, r=2)
         for t0 in range(0, N_BLOCKS, 4):
             nc.sync.dma_start(out=k_raw[:, t0 : t0 + 4, :], in_=k_view[:, t0 : t0 + 4, :])
         for t0 in range(0, N_BLOCKS, 4):
@@ -68,7 +71,10 @@ def tile_gatconv_pa_kernel(tc, X, A, Q, K, Wv, out):
             in_=Wv.rearrange("(u p e) n -> p u (e n)", u=2, p=P, e=2),
         )
         for t0 in range(0, N_BLOCKS, 4):
-            nc.sync.dma_start(out=x_raw[:, t0 : t0 + 4, :], in_=x_view[:, t0 : t0 + 4, :])
+            nc.sync.dma_start(
+                out=x_raw[:, t0 : t0 + 4, :].rearrange("p (v r) f -> p v (r f)", r=2),
+                in_=x_view[:, t0 // 2 : t0 // 2 + 2, :],
+            )
 
         block = {b: {} for b in range(N_BLOCKS)}
 
@@ -80,21 +86,49 @@ def tile_gatconv_pa_kernel(tc, X, A, Q, K, Wv, out):
             block[b]["edges"] = a_blk[:, :, 0]
             block[b]["edges_u32"] = a_blk[:].bitcast(U32)[:, :, 0]
 
-        for b in range(3):
+        for b in range(AHEAD):
             load_adjacency(b)
 
         ident_bf = keep.tile([P, P], BF16)
         make_identity(nc, ident_bf[:])
         ident_f32 = keep.tile([P, P], F32)
         make_identity(nc, ident_f32[:])
+        no_edge_ident = keep.tile([P, P], BF16)
+        nc.vector.tensor_scalar(
+            out=no_edge_ident[:], in0=ident_bf[:], scalar1=NO_EDGE, scalar2=None, op0=ALU.mult
+        )
+        minus_ident = keep.tile([P, P], BF16)
+        nc.vector.tensor_scalar(
+            out=minus_ident[:], in0=ident_bf[:], scalar1=-1.0, scalar2=None, op0=ALU.mult
+        )
         off_diagonal = keep.tile([P, P], BF16)
         nc.vector.tensor_scalar(
             out=off_diagonal[:], in0=ident_bf[:], scalar1=-1.0, scalar2=1.0, op0=ALU.mult, op1=ALU.add
         )
 
+        shifts = keep.tile([P, N_BLOCKS], F32)
+        folded = keep.tile([P, N_BLOCKS, 33], F32)
+        nc.gpsimd.memset(folded[:, :, 32:33], -SELF_SCORE)
+
+        def self_products(t0):
+            products = stage.tile([P, 4, D_HID], F32)
+            nc.gpsimd.tensor_tensor(
+                out=products[:], in0=q_raw[:, t0 : t0 + 4, :], in1=k_raw[:, t0 : t0 + 4, :], op=ALU.mult
+            )
+            for width in (128, 64, 32):
+                dst = products[:, :, :width] if width > 32 else folded[:, t0 : t0 + 4, :32]
+                nc.gpsimd.tensor_tensor(
+                    out=dst, in0=products[:, :, :width], in1=products[:, :, width : 2 * width], op=ALU.add
+                )
+
+        def self_scores(t0):
+            nc.vector.tensor_reduce(
+                out=shifts[:, t0 : t0 + 4], in_=folded[:, t0 : t0 + 4, :], axis=AXIS_X, op=ALU.add
+            )
+
         kT = keep.tile([P, H_HALVES, N_NODES], BF16)
         qT = keep.tile([P, H_HALVES, N_NODES], BF16)
-        for raw, flipped in ((k_raw, kT), (q_raw, qT)):
+        def flip(raw, flipped):
             for t0 in range(0, N_BLOCKS, 4):
                 flip_ps = psum_t.tile([P, H_HALVES, 4, P], BF16, tag="t")
                 for half in range(H_HALVES):
@@ -102,14 +136,18 @@ def tile_gatconv_pa_kernel(tc, X, A, Q, K, Wv, out):
                         nc.tensor.transpose(
                             flip_ps[:, half, a, :], raw[:, t0 + a, half * P : (half + 1) * P], ident_bf[:]
                         )
-                copy_out(
-                    t0 // 4,
-                    flipped[:, :, t0 * P : (t0 + 4) * P],
-                    flip_ps[:].rearrange("p h a j -> p h (a j)"),
-                )
+                dst = flipped[:, :, t0 * P : (t0 + 4) * P]
+                src = flip_ps[:].rearrange("p h a j -> p h (a j)")
+                if flipped is kT:
+                    copy_out(t0 // 4, dst, src)
+                else:
+                    nc.vector.tensor_scalar(out=dst, in0=src, scalar1=-1.0, scalar2=None, op0=ALU.mult)
 
         wv_grouped = keep.tile([P, D_OUT, PACK], BF16, align_bytes=64)
-        nc.vector.tensor_copy(out=wv_grouped[:], in_=wv_raw[:].rearrange("p t n -> p n t"))
+
+        def group_weights():
+            nc.vector.tensor_copy(out=wv_grouped[:], in_=wv_raw[:].rearrange("p t n -> p n t"))
+
         wv_codes = keep.tile([P, D_OUT], U32, align_bytes=64)
         wv_scales = keep.tile([P, D_OUT], U8, align_bytes=64)
 
@@ -121,28 +159,32 @@ def tile_gatconv_pa_kernel(tc, X, A, Q, K, Wv, out):
         v_grouped = keep.tile([P, N_PASSES, D_OUT, PACK], BF16, align_bytes=64)
         v_codes = keep.tile([P, N_PASSES, D_OUT], U32, align_bytes=64)
         v_scales = keep.tile([P, N_PASSES, D_OUT], U8, align_bytes=64)
-        for t0 in range(0, N_BLOCKS, 2):
+        def flip_x(t0):
             xt_ps = psum_t.tile([P, 2, 2, P], F32, tag="t")
             for a in range(2):
                 for u in range(2):
                     nc.tensor.transpose(xt_ps[:, a, u, :], x_words[:, t0 + a, u * P : (u + 1) * P], ident_f32[:])
-            copy_out(t0 // 2, x_grouped_words[:, t0 : t0 + 2, :, :], xt_ps[:].rearrange("p a u r -> p a r u"))
-        nc.vector.quantize_mx(
-            out=wv_codes[:].bitcast(FP8X4),
-            scales=wv_scales[:],
-            in_=wv_grouped[:].rearrange("p n t -> p (n t)"),
-        )
-        for g in range(N_PASSES):
+            nc.scalar.copy(out=x_grouped_words[:, t0 : t0 + 2, :, :], in_=xt_ps[:].rearrange("p a u r -> p a r u"))
+
+        def quantise_weights():
+            nc.vector.quantize_mx(
+                out=wv_codes[:].bitcast(FP8X4),
+                scales=wv_scales[:],
+                in_=wv_grouped[:].rearrange("p n t -> p (n t)"),
+            )
+
+        def quantise_x(g):
             tiles = slice(g * PACK, (g + 1) * PACK)
             nc.vector.quantize_mx(
                 out=x_codes[:, tiles, :].rearrange("p t r -> p (t r)").bitcast(FP8X4),
                 scales=x_scales[:, tiles, :].rearrange("p t r -> p (t r)"),
                 in_=x_grouped[:, tiles, :, :].rearrange("p t r k -> p (t r k)"),
             )
-        for g in range(N_PASSES):
+
+        def values(g):
             for half in range(D_OUT // P):
                 cols = slice(half * P, (half + 1) * P)
-                v_ps = psum_s.tile([P, PACK, P], F32, tag="s")
+                v_ps = psum_t.tile([P, PACK, P], F32, tag="t")
                 for t in range(PACK):
                     nc.tensor.matmul_mx(
                         out=v_ps[:, t, :],
@@ -153,95 +195,121 @@ def tile_gatconv_pa_kernel(tc, X, A, Q, K, Wv, out):
                         start=True,
                         stop=True,
                     )
-                copy_out(half, v_grouped[:, g, cols, :], v_ps[:].rearrange("p t d -> p d t"))
-        for g in range(N_PASSES):
+                nc.scalar.copy(out=v_grouped[:, g, cols, :], in_=v_ps[:].rearrange("p t d -> p d t"))
+
+        def quantise_values(g):
             nc.vector.quantize_mx(
                 out=v_codes[:, g, :].bitcast(FP8X4),
                 scales=v_scales[:, g, :],
                 in_=v_grouped[:, g, :, :].rearrange("p d t -> p (d t)"),
             )
 
-        def mask_on_scalar(b):
-            mask = stage.tile([P, N_NODES], BF16)
+        for b in range(N_BLOCKS):
+            own_chunk = b // (N_BLOCKS // N_CHUNKS)
+            block[b]["chunks"] = [own_chunk] + [c for c in range(N_CHUNKS) if c != own_chunk]
+
+        def own_mask(b):
+            own_chunk = block[b]["chunks"][0]
+            cols = slice(own_chunk * BANK, (own_chunk + 1) * BANK)
+            mask = stage.tile([P, BANK], BF16)
+            nc.scalar.activation(out=mask[:], in_=block[b]["edges_u32"][:, cols], func=ACT.Copy, scale=-1.0, bias=1.0)
+            first = b * P - own_chunk * BANK
+            own = mask[:, first : first + P]
+            nc.gpsimd.tensor_tensor(out=own, in0=own, in1=off_diagonal[:], op=ALU.mult)
             block[b]["mask"] = mask
-            nc.scalar.activation(
-                out=mask[:, VECTOR_COLS:],
-                in_=block[b]["edges_u32"][:, VECTOR_COLS:],
-                func=ACT.Copy,
-                scale=-NO_EDGE,
-                bias=NO_EDGE,
-            )
 
-        def mask_on_vector(b):
-            mask = block[b]["mask"]
-            nc.vector.tensor_scalar(
-                out=mask[:, :VECTOR_COLS],
-                in0=block[b]["edges"][:, :VECTOR_COLS],
-                scalar1=1.0,
-                scalar2=-NO_EDGE,
-                op0=ALU.subtract,
-                op1=ALU.mult,
-            )
-            own = mask[:, b * P : (b + 1) * P]
-            nc.vector.tensor_tensor(out=own, in0=own, in1=off_diagonal[:], op=ALU.mult)
-
-        def score_matmuls(b):
-            rows = slice(b * P, (b + 1) * P)
-            block[b]["s"] = []
-            for c in range(N_CHUNKS):
-                s_ps = psum_s.tile([P, BANK], F32, tag="s")
-                for half in range(H_HALVES):
-                    nc.tensor.matmul(
-                        out=s_ps[:],
-                        lhsT=qT[:, half, rows],
-                        rhs=kT[:, half, c * BANK : (c + 1) * BANK],
-                        start=(half == 0),
-                        stop=(half == H_HALVES - 1),
-                    )
-                block[b]["s"].append(s_ps)
-
-        def masked_scores(b):
-            z = stage.tile([P, N_NODES], F32)
-            for c in range(N_CHUNKS):
-                cols = slice(c * BANK, (c + 1) * BANK)
-                nc.vector.tensor_tensor(
-                    out=z[:, cols], in0=block[b]["s"][c][:], in1=block[b]["mask"][:, cols], op=ALU.add
+        def score_matmuls(b, chunk, own):
+            s_ps = psum_s.tile([P, BANK], F32, tag="s")
+            for half in range(H_HALVES):
+                nc.tensor.matmul(
+                    out=s_ps[:],
+                    lhsT=qT[:, half, b * P : (b + 1) * P],
+                    rhs=kT[:, half, chunk * BANK : (chunk + 1) * BANK],
+                    start=(half == 0),
+                    stop=(half == H_HALVES - 1 and not own),
                 )
-            neg_max = stats.tile([P, 1], F32)
-            nc.vector.tensor_reduce(out=neg_max[:], in_=z[:], axis=AXIS_X, op=ALU.max, negate=True)
+            if own:
+                nc.tensor.matmul(
+                    out=s_ps[:], lhsT=no_edge_ident[:], rhs=block[b]["mask"][:], start=False, stop=True
+                )
+            return s_ps
+
+        def other_scores(b):
+            block[b]["s"] = [score_matmuls(b, c, own=False) for c in block[b]["chunks"][1:]]
+
+        def own_scores(b):
+            block[b]["s_own"] = score_matmuls(b, block[b]["chunks"][0], own=True)
+
+        def mask_others(b):
+            z = zs.tile([P, N_CHUNKS, BANK], F32)
+            for k in range(1, N_CHUNKS):
+                c = block[b]["chunks"][k]
+                nc.vector.scalar_tensor_tensor(
+                    out=z[:, k, :],
+                    in0=block[b]["s"][k - 1][:],
+                    scalar=shifts[:, b : b + 1],
+                    in1=block[b]["edges"][:, c * BANK : (c + 1) * BANK],
+                    op0=ALU.add,
+                    op1=ALU.mult,
+                )
             block[b]["z"] = z
-            block[b]["neg_max"] = neg_max
+
+        def minimum_others(b):
+            others_min = stats.tile([P, 1], F32)
+            nc.vector.tensor_reduce(
+                out=others_min[:],
+                in_=block[b]["z"][:, 1:, :].rearrange("p c j -> p (c j)"),
+                axis=AXIS_X,
+                op=ALU.min,
+            )
+            block[b]["others_min"] = others_min
+
+        def move_own(b):
+            row_min = stats.tile([P, 1], F32)
+            nc.vector.tensor_scalar(
+                out=block[b]["z"][:, 0, :],
+                in0=block[b]["s_own"][:],
+                scalar1=shifts[:, b : b + 1],
+                scalar2=block[b]["others_min"][:],
+                op0=ALU.add,
+                op1=ALU.min,
+                accum_out=row_min[:],
+            )
+            block[b]["row_min"] = row_min
 
         def exponentials(b):
-            e_blk = stage.tile([P, N_NODES], BF16)
+            e_blk = stage.tile([P, N_CHUNKS, BANK], BF16)
             row_sum = stats.tile([P, 1], F32)
             nc.scalar.activation(
                 out=e_blk[:],
                 in_=block[b]["z"][:],
                 func=ACT.Exp,
-                bias=block[b]["neg_max"][:],
-                scale=1.0,
+                bias=block[b]["row_min"][:],
+                scale=-1.0,
                 accum_out=row_sum[:],
             )
             block[b]["e"] = e_blk
             block[b]["row_sum"] = row_sum
 
         def transposes(b):
+            e_words = block[b]["e"][:].bitcast(F32)
             block[b]["eT"] = []
             for g0 in range(0, N_PASSES, 2):
-                et_ps = psum_t.tile([P, 2, PACK, P], BF16, tag="t")
+                et_ps = psum_t.tile([P, 2, 2, P], F32, tag="t")
                 for a in range(2):
-                    for t in range(PACK):
-                        j0 = (g0 + a) * K_PASS + t * P
-                        nc.tensor.transpose(et_ps[:, a, t, :], block[b]["e"][:, j0 : j0 + P], ident_bf[:])
+                    for u in range(2):
+                        nc.tensor.transpose(
+                            et_ps[:, a, u, :], e_words[:, g0 + a, u * P : (u + 1) * P], ident_f32[:]
+                        )
                 block[b]["eT"].append(et_ps)
 
         def regroup(b):
             e_grouped = stage.tile([P, N_PASSES, P, PACK], BF16, align_bytes=64)
+            e_grouped_words = e_grouped[:].bitcast(F32)
             for g0 in range(0, N_PASSES, 2):
                 nc.scalar.copy(
-                    out=e_grouped[:, g0 : g0 + 2, :, :],
-                    in_=block[b]["eT"][g0 // 2][:].rearrange("p a t i -> p a i t"),
+                    out=e_grouped_words[:, g0 : g0 + 2, :, :],
+                    in_=block[b]["eT"][g0 // 2][:].rearrange("p a u i -> p a i u"),
                 )
             block[b]["e_grouped"] = e_grouped
 
@@ -266,8 +334,8 @@ def tile_gatconv_pa_kernel(tc, X, A, Q, K, Wv, out):
                     out=o_ps[:],
                     lhsT=block[b]["e_codes"][:, g, :].bitcast(FP8X4),
                     lhsT_scale=block[b]["e_scales"][:, g, :],
-                    rhs=v_codes[:, g, :].bitcast(FP8X4),
-                    rhs_scale=v_scales[:, g, :],
+                    rhs=v_codes[:, block[b]["chunks"][g], :].bitcast(FP8X4),
+                    rhs_scale=v_scales[:, block[b]["chunks"][g], :],
                     start=(g == 0),
                     stop=(g == N_PASSES - 1),
                 )
@@ -276,18 +344,53 @@ def tile_gatconv_pa_kernel(tc, X, A, Q, K, Wv, out):
         def finish(b):
             o_sb = stage.tile([P, D_OUT], F32)
             nc.scalar.activation(out=o_sb[:], in_=block[b]["o"][:], func=ACT.Copy, scale=block[b]["inv_sum"][:])
-            nc.gpsimd.dma_start(out=out[b * P : (b + 1) * P, :], in_=o_sb[:])
+            nc.sync.dma_start(out=out[b * P : (b + 1) * P, :], in_=o_sb[:])
 
-        for b in range(N_BLOCKS):
-            if b + 3 < N_BLOCKS:
-                load_adjacency(b + 3)
-            mask_on_scalar(b)
-            mask_on_vector(b)
-            score_matmuls(b)
-            masked_scores(b)
-            exponentials(b)
-            transposes(b)
-            regroup(b)
-            quantise(b)
-            weighted_sum(b)
-            finish(b)
+        with tc.manual_schedule():
+            self_products(0)
+            flip(k_raw, kT)
+            flip(q_raw, qT)
+            group_weights()
+            self_scores(0)
+            for t0 in range(0, N_BLOCKS, 2):
+                flip_x(t0)
+            quantise_weights()
+            for g in range(N_PASSES):
+                quantise_x(g)
+            own_mask(0)
+            other_scores(0)
+            own_scores(0)
+            for b in range(N_BLOCKS + 3):
+                if b + AHEAD < N_BLOCKS:
+                    load_adjacency(b + AHEAD)
+                if b < N_BLOCKS:
+                    mask_others(b)
+                    minimum_others(b)
+                if b + 1 < N_BLOCKS:
+                    other_scores(b + 1)
+                if 0 <= b - 1 < N_BLOCKS:
+                    exponentials(b - 1)
+                    transposes(b - 1)
+                if b + 1 < N_BLOCKS:
+                    own_mask(b + 1)
+                if b < 3:
+                    self_products(4 * b + 4)
+                if 1 <= b <= 3:
+                    self_scores(4 * b)
+                if 0 <= b - 3 < N_BLOCKS:
+                    finish(b - 3)
+                if b < 2:
+                    values(2 * b)
+                    values(2 * b + 1)
+                if 0 <= b - 1 < N_BLOCKS:
+                    regroup(b - 1)
+                if b == 2:
+                    for g in range(N_PASSES):
+                        quantise_values(g)
+                if 0 <= b - 2 < N_BLOCKS:
+                    quantise(b - 2)
+                    weighted_sum(b - 2)
+                if b < N_BLOCKS:
+                    move_own(b)
+                if b + 1 < N_BLOCKS:
+                    own_scores(b + 1)

@@ -32,6 +32,9 @@ NO_EDGE = 2.0**126
 
 SELF_SCORE = 48.0
 
+OWN = N_CHUNKS - 1
+Z_FIRST = 4
+
 AHEAD = 4
 
 FLOPS = 2 * N_NODES * (D_IN * D_OUT + N_NODES * D_HID + N_NODES * D_OUT)
@@ -42,18 +45,13 @@ def tile_gatconv_pa_kernel(tc, X, A, Q, K, Wv, out):
     with ExitStack() as stack:
         keep = stack.enter_context(tc.tile_pool(name="keep", bufs=1))
         stage = stack.enter_context(tc.tile_pool(name="stage", bufs=3))
-        zs = stack.enter_context(tc.tile_pool(name="zs", bufs=3))
+        codes = stack.enter_context(tc.tile_pool(name="codes", bufs=5))
+        zs = stack.enter_context(tc.tile_pool(name="zs", bufs=2))
         stats = stack.enter_context(tc.tile_pool(name="stats", bufs=4))
         adjacency = stack.enter_context(tc.tile_pool(name="adjacency", bufs=4))
         psum_s = stack.enter_context(tc.psum_pool(name="psum_s", bufs=4))
-        psum_t = stack.enter_context(tc.psum_pool(name="psum_t", bufs=3))
-        psum_o = stack.enter_context(tc.psum_pool(name="psum_o", bufs=1))
-
-        def copy_out(piece, dst, src):
-            if piece % 2 == 0:
-                nc.scalar.copy(out=dst, in_=src)
-            else:
-                nc.vector.tensor_copy(out=dst, in_=src)
+        psum_t = stack.enter_context(tc.psum_pool(name="psum_t", bufs=2))
+        psum_o = stack.enter_context(tc.psum_pool(name="psum_o", bufs=2))
 
         k_raw = keep.tile([P, N_BLOCKS, D_HID], BF16)
         q_raw = keep.tile([P, N_BLOCKS, D_HID], BF16)
@@ -65,17 +63,6 @@ def tile_gatconv_pa_kernel(tc, X, A, Q, K, Wv, out):
             nc.sync.dma_start(out=k_raw[:, t0 : t0 + 4, :], in_=k_view[:, t0 : t0 + 4, :])
         for t0 in range(0, N_BLOCKS, 4):
             nc.sync.dma_start(out=q_raw[:, t0 : t0 + 4, :], in_=q_view[:, t0 : t0 + 4, :])
-        wv_raw = keep.tile([P, PACK, D_OUT], BF16)
-        nc.sync.dma_start(
-            out=wv_raw[:].rearrange("p (u e) n -> p u (e n)", u=2),
-            in_=Wv.rearrange("(u p e) n -> p u (e n)", u=2, p=P, e=2),
-        )
-        for t0 in range(0, N_BLOCKS, 4):
-            nc.sync.dma_start(
-                out=x_raw[:, t0 : t0 + 4, :].rearrange("p (v r) f -> p v (r f)", r=2),
-                in_=x_view[:, t0 // 2 : t0 // 2 + 2, :],
-            )
-
         block = {b: {} for b in range(N_BLOCKS)}
 
         def load_adjacency(b):
@@ -86,6 +73,20 @@ def tile_gatconv_pa_kernel(tc, X, A, Q, K, Wv, out):
             block[b]["edges"] = a_blk[:, :, 0]
             block[b]["edges_u32"] = a_blk[:].bitcast(U32)[:, :, 0]
 
+        wv_raw = keep.tile([P, PACK, D_OUT], BF16)
+        nc.sync.dma_start(
+            out=wv_raw[:].rearrange("p (u e) n -> p u (e n)", u=2),
+            in_=Wv.rearrange("(u p e) n -> p u (e n)", u=2, p=P, e=2),
+        )
+
+        def load_x(t0):
+            nc.sync.dma_start(
+                out=x_raw[:, t0 : t0 + 4, :].rearrange("p (v r) f -> p v (r f)", r=2),
+                in_=x_view[:, t0 // 2 : t0 // 2 + 2, :],
+            )
+
+        for t0 in range(0, N_BLOCKS, 4):
+            load_x(t0)
         for b in range(AHEAD):
             load_adjacency(b)
 
@@ -111,12 +112,12 @@ def tile_gatconv_pa_kernel(tc, X, A, Q, K, Wv, out):
         nc.gpsimd.memset(folded[:, :, 32:33], -SELF_SCORE)
 
         def self_products(t0):
-            products = stage.tile([P, 4, D_HID], F32)
+            products = stage.tile([P, 2, D_HID], F32)
             nc.gpsimd.tensor_tensor(
-                out=products[:], in0=q_raw[:, t0 : t0 + 4, :], in1=k_raw[:, t0 : t0 + 4, :], op=ALU.mult
+                out=products[:], in0=q_raw[:, t0 : t0 + 2, :], in1=k_raw[:, t0 : t0 + 2, :], op=ALU.mult
             )
             for width in (128, 64, 32):
-                dst = products[:, :, :width] if width > 32 else folded[:, t0 : t0 + 4, :32]
+                dst = products[:, :, :width] if width > 32 else folded[:, t0 : t0 + 2, :32]
                 nc.gpsimd.tensor_tensor(
                     out=dst, in0=products[:, :, :width], in1=products[:, :, width : 2 * width], op=ALU.add
                 )
@@ -128,20 +129,20 @@ def tile_gatconv_pa_kernel(tc, X, A, Q, K, Wv, out):
 
         kT = keep.tile([P, H_HALVES, N_NODES], BF16)
         qT = keep.tile([P, H_HALVES, N_NODES], BF16)
-        def flip(raw, flipped):
-            for t0 in range(0, N_BLOCKS, 4):
-                flip_ps = psum_t.tile([P, H_HALVES, 4, P], BF16, tag="t")
-                for half in range(H_HALVES):
-                    for a in range(4):
-                        nc.tensor.transpose(
-                            flip_ps[:, half, a, :], raw[:, t0 + a, half * P : (half + 1) * P], ident_bf[:]
-                        )
-                dst = flipped[:, :, t0 * P : (t0 + 4) * P]
-                src = flip_ps[:].rearrange("p h a j -> p h (a j)")
-                if flipped is kT:
-                    copy_out(t0 // 4, dst, src)
-                else:
-                    nc.vector.tensor_scalar(out=dst, in0=src, scalar1=-1.0, scalar2=None, op0=ALU.mult)
+        def flip(raw, flipped, t0):
+            pool, tag = (psum_s, "s") if flipped is kT else (psum_o, "o")
+            flip_ps = pool.tile([P, H_HALVES, 4, P], BF16, tag=tag)
+            for half in range(H_HALVES):
+                for a in range(4):
+                    nc.tensor.transpose(
+                        flip_ps[:, half, a, :], raw[:, t0 + a, half * P : (half + 1) * P], ident_bf[:]
+                    )
+            dst = flipped[:, :, t0 * P : (t0 + 4) * P]
+            src = flip_ps[:].rearrange("p h a j -> p h (a j)")
+            if flipped is kT:
+                nc.vector.tensor_copy(out=dst, in_=src)
+            else:
+                nc.vector.tensor_scalar(out=dst, in0=src, scalar1=-1.0, scalar2=None, op0=ALU.mult)
 
         wv_grouped = keep.tile([P, D_OUT, PACK], BF16, align_bytes=64)
 
@@ -206,10 +207,10 @@ def tile_gatconv_pa_kernel(tc, X, A, Q, K, Wv, out):
 
         for b in range(N_BLOCKS):
             own_chunk = b // (N_BLOCKS // N_CHUNKS)
-            block[b]["chunks"] = [own_chunk] + [c for c in range(N_CHUNKS) if c != own_chunk]
+            block[b]["chunks"] = [c for c in range(N_CHUNKS) if c != own_chunk] + [own_chunk]
 
         def own_mask(b):
-            own_chunk = block[b]["chunks"][0]
+            own_chunk = block[b]["chunks"][OWN]
             cols = slice(own_chunk * BANK, (own_chunk + 1) * BANK)
             mask = stage.tile([P, BANK], BF16)
             nc.scalar.activation(out=mask[:], in_=block[b]["edges_u32"][:, cols], func=ACT.Copy, scale=-1.0, bias=1.0)
@@ -234,19 +235,19 @@ def tile_gatconv_pa_kernel(tc, X, A, Q, K, Wv, out):
                 )
             return s_ps
 
-        def other_scores(b):
-            block[b]["s"] = [score_matmuls(b, c, own=False) for c in block[b]["chunks"][1:]]
+        def other_scores(b, k):
+            block[b]["s", k] = score_matmuls(b, block[b]["chunks"][k], own=False)
 
         def own_scores(b):
-            block[b]["s_own"] = score_matmuls(b, block[b]["chunks"][0], own=True)
+            block[b]["s", OWN] = score_matmuls(b, block[b]["chunks"][OWN], own=True)
 
         def mask_others(b):
-            z = zs.tile([P, N_CHUNKS, BANK], F32)
-            for k in range(1, N_CHUNKS):
+            z = zs.tile([P, Z_FIRST + N_NODES], F32)
+            for k in range(OWN):
                 c = block[b]["chunks"][k]
                 nc.vector.scalar_tensor_tensor(
-                    out=z[:, k, :],
-                    in0=block[b]["s"][k - 1][:],
+                    out=z[:, Z_FIRST + k * BANK : Z_FIRST + (k + 1) * BANK],
+                    in0=block[b]["s", k][:],
                     scalar=shifts[:, b : b + 1],
                     in1=block[b]["edges"][:, c * BANK : (c + 1) * BANK],
                     op0=ALU.add,
@@ -254,81 +255,84 @@ def tile_gatconv_pa_kernel(tc, X, A, Q, K, Wv, out):
                 )
             block[b]["z"] = z
 
-        def minimum_others(b):
-            others_min = stats.tile([P, 1], F32)
+        def move_own(b):
+            nc.vector.tensor_scalar(
+                out=block[b]["z"][:, Z_FIRST + OWN * BANK :],
+                in0=block[b]["s", OWN][:],
+                scalar1=shifts[:, b : b + 1],
+                scalar2=None,
+                op0=ALU.add,
+                op1=ALU.min,
+                accum_out=block[b]["z"][:, Z_FIRST - 1 : Z_FIRST],
+            )
+
+        def minimum(b):
+            row_min = stats.tile([P, 1], F32)
             nc.vector.tensor_reduce(
-                out=others_min[:],
-                in_=block[b]["z"][:, 1:, :].rearrange("p c j -> p (c j)"),
+                out=row_min[:],
+                in_=block[b]["z"][:, Z_FIRST - 1 : Z_FIRST + OWN * BANK],
                 axis=AXIS_X,
                 op=ALU.min,
             )
-            block[b]["others_min"] = others_min
-
-        def move_own(b):
-            row_min = stats.tile([P, 1], F32)
-            nc.vector.tensor_scalar(
-                out=block[b]["z"][:, 0, :],
-                in0=block[b]["s_own"][:],
-                scalar1=shifts[:, b : b + 1],
-                scalar2=block[b]["others_min"][:],
-                op0=ALU.add,
-                op1=ALU.min,
-                accum_out=row_min[:],
-            )
             block[b]["row_min"] = row_min
 
-        def exponentials(b):
-            e_blk = stage.tile([P, N_CHUNKS, BANK], BF16)
-            row_sum = stats.tile([P, 1], F32)
+        def exponentials(b, slots, part):
+            if part == 0:
+                e_blk = stage.tile([P, N_CHUNKS, BANK], BF16)
+                row_sums = stats.tile([P, 2], F32)
+                block[b]["e"] = e_blk
+                block[b]["row_sums"] = row_sums
             nc.scalar.activation(
-                out=e_blk[:],
-                in_=block[b]["z"][:],
+                out=block[b]["e"][:, slots, :].rearrange("p c j -> p (c j)"),
+                in_=block[b]["z"][:, Z_FIRST + slots.start * BANK : Z_FIRST + slots.stop * BANK],
                 func=ACT.Exp,
                 bias=block[b]["row_min"][:],
                 scale=-1.0,
-                accum_out=row_sum[:],
+                accum_out=block[b]["row_sums"][:, part : part + 1],
             )
-            block[b]["e"] = e_blk
-            block[b]["row_sum"] = row_sum
 
-        def transposes(b):
+        def transposes(b, g0):
             e_words = block[b]["e"][:].bitcast(F32)
-            block[b]["eT"] = []
-            for g0 in range(0, N_PASSES, 2):
-                et_ps = psum_t.tile([P, 2, 2, P], F32, tag="t")
-                for a in range(2):
-                    for u in range(2):
-                        nc.tensor.transpose(
-                            et_ps[:, a, u, :], e_words[:, g0 + a, u * P : (u + 1) * P], ident_f32[:]
-                        )
-                block[b]["eT"].append(et_ps)
+            et_ps = psum_t.tile([P, 2, 2, P], F32, tag="t")
+            for a in range(2):
+                for u in range(2):
+                    nc.tensor.transpose(et_ps[:, a, u, :], e_words[:, g0 + a, u * P : (u + 1) * P], ident_f32[:])
+            block[b]["eT", g0] = et_ps
 
-        def regroup(b):
-            e_grouped = stage.tile([P, N_PASSES, P, PACK], BF16, align_bytes=64)
-            e_grouped_words = e_grouped[:].bitcast(F32)
-            for g0 in range(0, N_PASSES, 2):
-                nc.scalar.copy(
-                    out=e_grouped_words[:, g0 : g0 + 2, :, :],
-                    in_=block[b]["eT"][g0 // 2][:].rearrange("p a u i -> p a i u"),
-                )
-            block[b]["e_grouped"] = e_grouped
-
-        def quantise(b):
-            e_codes = stage.tile([P, N_PASSES, P], U32, align_bytes=64)
-            e_scales = stage.tile([P, N_PASSES, P], U8, align_bytes=64)
-            nc.vector.quantize_mx(
-                out=e_codes[:].rearrange("p g i -> p (g i)").bitcast(FP8X4),
-                scales=e_scales[:].rearrange("p g i -> p (g i)"),
-                in_=block[b]["e_grouped"][:].rearrange("p g i t -> p (g i t)"),
+        def regroup(b, g0):
+            if g0 == 0:
+                e_grouped = stage.tile([P, N_PASSES, P, PACK], BF16, align_bytes=64)
+                block[b]["e_grouped"] = e_grouped
+            e_grouped_words = block[b]["e_grouped"][:].bitcast(F32)
+            nc.scalar.copy(
+                out=e_grouped_words[:, g0 : g0 + 2, :, :],
+                in_=block[b]["eT", g0][:].rearrange("p a u i -> p a i u"),
             )
-            block[b]["e_codes"] = e_codes
-            block[b]["e_scales"] = e_scales
-            inv_sum = stats.tile([P, 1], F32)
-            nc.vector.reciprocal(out=inv_sum[:], in_=block[b]["row_sum"][:])
+
+        def quantise(b, passes):
+            if passes.start == 0:
+                e_codes = codes.tile([P, N_PASSES, P], U32, align_bytes=64)
+                e_scales = codes.tile([P, N_PASSES, P], U8, align_bytes=64)
+                block[b]["e_codes"] = e_codes
+                block[b]["e_scales"] = e_scales
+            nc.vector.quantize_mx(
+                out=block[b]["e_codes"][:, passes, :].rearrange("p g i -> p (g i)").bitcast(FP8X4),
+                scales=block[b]["e_scales"][:, passes, :].rearrange("p g i -> p (g i)"),
+                in_=block[b]["e_grouped"][:, passes, :, :].rearrange("p g i t -> p (g i t)"),
+            )
+
+        def invert(b, parts):
+            row_sums = block[b]["row_sums"]
+            if parts == 2:
+                nc.vector.tensor_tensor(
+                    out=row_sums[:, 0:1], in0=row_sums[:, 0:1], in1=row_sums[:, 1:2], op=ALU.add
+                )
+            inv_sum = codes.tile([P, 1], F32)
+            nc.vector.reciprocal(out=inv_sum[:], in_=row_sums[:, 0:1])
             block[b]["inv_sum"] = inv_sum
 
         def weighted_sum(b):
-            o_ps = psum_o.tile([P, D_OUT], F32)
+            o_ps = psum_o.tile([P, D_OUT], F32, tag="o")
             for g in range(N_PASSES):
                 nc.tensor.matmul_mx(
                     out=o_ps[:],
@@ -346,51 +350,81 @@ def tile_gatconv_pa_kernel(tc, X, A, Q, K, Wv, out):
             nc.scalar.activation(out=o_sb[:], in_=block[b]["o"][:], func=ACT.Copy, scale=block[b]["inv_sum"][:])
             nc.sync.dma_start(out=out[b * P : (b + 1) * P, :], in_=o_sb[:])
 
+        every = slice(0, N_CHUNKS)
+        first_half, second_half = slice(0, 2), slice(2, N_CHUNKS)
+        last = N_BLOCKS - 1
         with tc.manual_schedule():
-            self_products(0)
-            flip(k_raw, kT)
-            flip(q_raw, qT)
+            for t0 in range(0, 6, 2):
+                self_products(t0)
+            for t0 in range(0, N_BLOCKS, 4):
+                flip(k_raw, kT, t0)
+            flip(q_raw, qT, 0)
+            flip(q_raw, qT, 4)
             group_weights()
-            self_scores(0)
-            for t0 in range(0, N_BLOCKS, 2):
-                flip_x(t0)
             quantise_weights()
             for g in range(N_PASSES):
+                flip_x(4 * g)
+                flip_x(4 * g + 2)
+                if g < 2:
+                    flip(q_raw, qT, 4 * g + 8)
+                else:
+                    other_scores(0, g - 2)
                 quantise_x(g)
+            other_scores(0, 2)
+            self_scores(0)
+            values(0)
             own_mask(0)
-            other_scores(0)
+            values(1)
             own_scores(0)
-            for b in range(N_BLOCKS + 3):
+            for b in range(N_BLOCKS + 1):
                 if b + AHEAD < N_BLOCKS:
                     load_adjacency(b + AHEAD)
                 if b < N_BLOCKS:
                     mask_others(b)
-                    minimum_others(b)
-                if b + 1 < N_BLOCKS:
-                    other_scores(b + 1)
-                if 0 <= b - 1 < N_BLOCKS:
-                    exponentials(b - 1)
-                    transposes(b - 1)
-                if b + 1 < N_BLOCKS:
-                    own_mask(b + 1)
-                if b < 3:
-                    self_products(4 * b + 4)
-                if 1 <= b <= 3:
-                    self_scores(4 * b)
-                if 0 <= b - 3 < N_BLOCKS:
-                    finish(b - 3)
-                if b < 2:
-                    values(2 * b)
-                    values(2 * b + 1)
-                if 0 <= b - 1 < N_BLOCKS:
-                    regroup(b - 1)
-                if b == 2:
-                    for g in range(N_PASSES):
-                        quantise_values(g)
-                if 0 <= b - 2 < N_BLOCKS:
-                    quantise(b - 2)
-                    weighted_sum(b - 2)
-                if b < N_BLOCKS:
                     move_own(b)
                 if b + 1 < N_BLOCKS:
+                    for k in range(OWN):
+                        other_scores(b + 1, k)
+                        if b == 0 and k < 2:
+                            values(k + 2)
+                if 1 <= b < N_BLOCKS:
+                    exponentials(b - 1, every, 0)
+                    transposes(b - 1, 0)
+                    transposes(b - 1, 2)
+                if b < 5:
+                    self_products(2 * b + 6)
+                if b + 1 < N_BLOCKS:
+                    own_mask(b + 1)
+                if b in (3, 7, 11):
+                    self_scores(b + 1)
+                if 3 <= b < N_BLOCKS:
+                    finish(b - 3)
+                if 1 <= b < N_BLOCKS:
+                    regroup(b - 1, 0)
+                    regroup(b - 1, 2)
+                if b == 1 or b == 2:
+                    quantise_values(2 * b - 2)
+                    quantise_values(2 * b - 1)
+                if b == last:
+                    minimum(b)
+                if b >= 2:
+                    quantise(b - 2, every)
+                    invert(b - 2, 1)
+                    weighted_sum(b - 2)
+                if b + 1 < N_BLOCKS:
                     own_scores(b + 1)
+                if b < last:
+                    minimum(b)
+            exponentials(last, first_half, 0)
+            exponentials(last, second_half, 1)
+            transposes(last, 0)
+            transposes(last, 2)
+            regroup(last, 0)
+            regroup(last, 2)
+            finish(last - 2)
+            finish(last - 1)
+            quantise(last, first_half)
+            invert(last, 2)
+            quantise(last, second_half)
+            weighted_sum(last)
+            finish(last)

@@ -59,25 +59,13 @@ def tile_gatconv_pa_kernel(tc, X, A, Q, K, Wv, out):
         k_view = K.rearrange("(t p) h -> p t h", p=P)
         q_view = Q.rearrange("(t p) h -> p t h", p=P)
         x_view = X.rearrange("(v p r) f -> p v (r f)", p=P, r=2)
-        for t0 in range(0, N_BLOCKS, 4):
-            nc.sync.dma_start(out=k_raw[:, t0 : t0 + 4, :], in_=k_view[:, t0 : t0 + 4, :])
-        for t0 in range(0, N_BLOCKS, 4):
-            nc.sync.dma_start(out=q_raw[:, t0 : t0 + 4, :], in_=q_view[:, t0 : t0 + 4, :])
-        block = {b: {} for b in range(N_BLOCKS)}
-
-        def load_adjacency(b):
-            a_blk = adjacency.tile([P, N_NODES, 2], I32)
-            nc.sync.dma_start(
-                out=a_blk[:].rearrange("p j w -> p (j w)"), in_=A.bitcast(I32)[b * P : (b + 1) * P, :]
-            )
-            block[b]["edges"] = a_blk[:, :, 0]
-            block[b]["edges_u32"] = a_blk[:].bitcast(U32)[:, :, 0]
-
         wv_raw = keep.tile([P, PACK, D_OUT], BF16)
-        nc.sync.dma_start(
-            out=wv_raw[:].rearrange("p (u e) n -> p u (e n)", u=2),
-            in_=Wv.rearrange("(u p e) n -> p u (e n)", u=2, p=P, e=2),
-        )
+
+        def load_k(t0):
+            nc.sync.dma_start(out=k_raw[:, t0 : t0 + 4, :], in_=k_view[:, t0 : t0 + 4, :])
+
+        def load_q(t0):
+            nc.sync.dma_start(out=q_raw[:, t0 : t0 + 4, :], in_=q_view[:, t0 : t0 + 4, :])
 
         def load_x(t0):
             nc.sync.dma_start(
@@ -85,11 +73,44 @@ def tile_gatconv_pa_kernel(tc, X, A, Q, K, Wv, out):
                 in_=x_view[:, t0 // 2 : t0 // 2 + 2, :],
             )
 
+        def load_weights():
+            nc.sync.dma_start(
+                out=wv_raw[:].rearrange("p (u e) n -> p u (e n)", u=2),
+                in_=Wv.rearrange("(u p e) n -> p u (e n)", u=2, p=P, e=2),
+            )
+
+        block = {b: {} for b in range(N_BLOCKS)}
+
+        for b in range(N_BLOCKS):
+            own_chunk = b // (N_BLOCKS // N_CHUNKS)
+            block[b]["chunks"] = [c for c in range(N_CHUNKS) if c != own_chunk] + [own_chunk]
+
+        def load_adjacency(b):
+            a_blk = adjacency.tile([P, N_NODES, 2], I32)
+            order = block[b]["chunks"][OWN:] + block[b]["chunks"][:OWN]
+            pieces = [slice(c * BANK, (c + 1) * BANK) for c in order] if b < 2 else [slice(0, N_NODES)]
+            for cols in pieces:
+                nc.sync.dma_start(
+                    out=a_blk[:, cols, :].rearrange("p j w -> p (j w)"),
+                    in_=A.bitcast(I32)[b * P : (b + 1) * P, 2 * cols.start : 2 * cols.stop],
+                )
+            block[b]["edges"] = a_blk[:, :, 0]
+            block[b]["edges_u32"] = a_blk[:].bitcast(U32)[:, :, 0]
+
+        load_k(0)
+        load_q(0)
+        for t0 in range(4, N_BLOCKS, 4):
+            load_k(t0)
+        load_weights()
         for t0 in range(0, N_BLOCKS, 4):
             load_x(t0)
-        for b in range(AHEAD):
-            load_adjacency(b)
-
+        load_adjacency(0)
+        load_adjacency(1)
+        load_q(4)
+        load_adjacency(2)
+        load_q(8)
+        load_q(12)
+        load_adjacency(3)
         ident_bf = keep.tile([P, P], BF16)
         make_identity(nc, ident_bf[:])
         ident_f32 = keep.tile([P, P], F32)
@@ -111,38 +132,51 @@ def tile_gatconv_pa_kernel(tc, X, A, Q, K, Wv, out):
         folded = keep.tile([P, N_BLOCKS, 33], F32)
         nc.gpsimd.memset(folded[:, :, 32:33], -SELF_SCORE)
 
-        def self_products(t0):
+        def self_products(t0, n):
             products = stage.tile([P, 2, D_HID], F32)
+            tiles = slice(t0, t0 + n)
             nc.gpsimd.tensor_tensor(
-                out=products[:], in0=q_raw[:, t0 : t0 + 2, :], in1=k_raw[:, t0 : t0 + 2, :], op=ALU.mult
+                out=products[:, :n, :], in0=q_raw[:, tiles, :], in1=k_raw[:, tiles, :], op=ALU.mult
             )
             for width in (128, 64, 32):
-                dst = products[:, :, :width] if width > 32 else folded[:, t0 : t0 + 2, :32]
+                dst = products[:, :n, :width] if width > 32 else folded[:, tiles, :32]
                 nc.gpsimd.tensor_tensor(
-                    out=dst, in0=products[:, :, :width], in1=products[:, :, width : 2 * width], op=ALU.add
+                    out=dst, in0=products[:, :n, :width], in1=products[:, :n, width : 2 * width], op=ALU.add
                 )
 
-        def self_scores(t0):
+        def self_scores(t0, n):
             nc.vector.tensor_reduce(
-                out=shifts[:, t0 : t0 + 4], in_=folded[:, t0 : t0 + 4, :], axis=AXIS_X, op=ALU.add
+                out=shifts[:, t0 : t0 + n], in_=folded[:, t0 : t0 + n, :], axis=AXIS_X, op=ALU.add
             )
+
+        def first_self_score():
+            products = keep.tile([P, D_HID + 1], F32)
+            nc.vector.memset(products[:, D_HID:], -SELF_SCORE)
+            nc.vector.tensor_tensor(out=products[:, :D_HID], in0=q_raw[:, 0, :], in1=k_raw[:, 0, :], op=ALU.mult)
+            nc.vector.tensor_reduce(out=shifts[:, 0:1], in_=products[:], axis=AXIS_X, op=ALU.add)
 
         kT = keep.tile([P, H_HALVES, N_NODES], BF16)
         qT = keep.tile([P, H_HALVES, N_NODES], BF16)
-        def flip(raw, flipped, t0):
-            pool, tag = (psum_s, "s") if flipped is kT else (psum_o, "o")
+        def flip_transposes(raw, flipped, t0):
+            pool, tag = (psum_t, "t") if flipped is kT else (psum_o, "o")
             flip_ps = pool.tile([P, H_HALVES, 4, P], BF16, tag=tag)
             for half in range(H_HALVES):
                 for a in range(4):
                     nc.tensor.transpose(
                         flip_ps[:, half, a, :], raw[:, t0 + a, half * P : (half + 1) * P], ident_bf[:]
                     )
+            return flip_ps
+
+        def flip_copy(flip_ps, flipped, t0):
             dst = flipped[:, :, t0 * P : (t0 + 4) * P]
             src = flip_ps[:].rearrange("p h a j -> p h (a j)")
             if flipped is kT:
                 nc.vector.tensor_copy(out=dst, in_=src)
             else:
                 nc.vector.tensor_scalar(out=dst, in0=src, scalar1=-1.0, scalar2=None, op0=ALU.mult)
+
+        def flip(raw, flipped, t0):
+            flip_copy(flip_transposes(raw, flipped, t0), flipped, t0)
 
         wv_grouped = keep.tile([P, D_OUT, PACK], BF16, align_bytes=64)
 
@@ -185,7 +219,7 @@ def tile_gatconv_pa_kernel(tc, X, A, Q, K, Wv, out):
         def values(g):
             for half in range(D_OUT // P):
                 cols = slice(half * P, (half + 1) * P)
-                v_ps = psum_t.tile([P, PACK, P], F32, tag="t")
+                v_ps = psum_o.tile([P, PACK, P], F32, tag="o")
                 for t in range(PACK):
                     nc.tensor.matmul_mx(
                         out=v_ps[:, t, :],
@@ -204,10 +238,6 @@ def tile_gatconv_pa_kernel(tc, X, A, Q, K, Wv, out):
                 scales=v_scales[:, g, :],
                 in_=v_grouped[:, g, :, :].rearrange("p d t -> p (d t)"),
             )
-
-        for b in range(N_BLOCKS):
-            own_chunk = b // (N_BLOCKS // N_CHUNKS)
-            block[b]["chunks"] = [c for c in range(N_CHUNKS) if c != own_chunk] + [own_chunk]
 
         def own_mask(b):
             own_chunk = block[b]["chunks"][OWN]
@@ -241,19 +271,20 @@ def tile_gatconv_pa_kernel(tc, X, A, Q, K, Wv, out):
         def own_scores(b):
             block[b]["s", OWN] = score_matmuls(b, block[b]["chunks"][OWN], own=True)
 
-        def mask_others(b):
+        def new_z(b):
             z = zs.tile([P, Z_FIRST + N_NODES], F32)
-            for k in range(OWN):
-                c = block[b]["chunks"][k]
-                nc.vector.scalar_tensor_tensor(
-                    out=z[:, Z_FIRST + k * BANK : Z_FIRST + (k + 1) * BANK],
-                    in0=block[b]["s", k][:],
-                    scalar=shifts[:, b : b + 1],
-                    in1=block[b]["edges"][:, c * BANK : (c + 1) * BANK],
-                    op0=ALU.add,
-                    op1=ALU.mult,
-                )
             block[b]["z"] = z
+
+        def mask_other(b, k):
+            c = block[b]["chunks"][k]
+            nc.vector.scalar_tensor_tensor(
+                out=block[b]["z"][:, Z_FIRST + k * BANK : Z_FIRST + (k + 1) * BANK],
+                in0=block[b]["s", k][:],
+                scalar=shifts[:, b : b + 1],
+                in1=block[b]["edges"][:, c * BANK : (c + 1) * BANK],
+                op0=ALU.add,
+                op1=ALU.mult,
+            )
 
         def move_own(b):
             nc.vector.tensor_scalar(
@@ -279,7 +310,7 @@ def tile_gatconv_pa_kernel(tc, X, A, Q, K, Wv, out):
         def exponentials(b, slots, part):
             if part == 0:
                 e_blk = stage.tile([P, N_CHUNKS, BANK], BF16)
-                row_sums = stats.tile([P, 2], F32)
+                row_sums = stats.tile([P, 3], F32)
                 block[b]["e"] = e_blk
                 block[b]["row_sums"] = row_sums
             nc.scalar.activation(
@@ -291,22 +322,22 @@ def tile_gatconv_pa_kernel(tc, X, A, Q, K, Wv, out):
                 accum_out=block[b]["row_sums"][:, part : part + 1],
             )
 
-        def transposes(b, g0):
+        def transposes(b, slots):
             e_words = block[b]["e"][:].bitcast(F32)
             et_ps = psum_t.tile([P, 2, 2, P], F32, tag="t")
-            for a in range(2):
+            for a, slot in enumerate(range(slots.start, slots.stop)):
                 for u in range(2):
-                    nc.tensor.transpose(et_ps[:, a, u, :], e_words[:, g0 + a, u * P : (u + 1) * P], ident_f32[:])
-            block[b]["eT", g0] = et_ps
+                    nc.tensor.transpose(et_ps[:, a, u, :], e_words[:, slot, u * P : (u + 1) * P], ident_f32[:])
+            block[b]["eT", slots.start] = et_ps
 
-        def regroup(b, g0):
-            if g0 == 0:
+        def regroup(b, slots, copy=nc.scalar.copy):
+            if slots.start == 0:
                 e_grouped = stage.tile([P, N_PASSES, P, PACK], BF16, align_bytes=64)
                 block[b]["e_grouped"] = e_grouped
             e_grouped_words = block[b]["e_grouped"][:].bitcast(F32)
-            nc.scalar.copy(
-                out=e_grouped_words[:, g0 : g0 + 2, :, :],
-                in_=block[b]["eT", g0][:].rearrange("p a u i -> p a i u"),
+            copy(
+                out=e_grouped_words[:, slots, :, :],
+                in_=block[b]["eT", slots.start][:, : slots.stop - slots.start, :, :].rearrange("p a u i -> p a i u"),
             )
 
         def quantise(b, passes):
@@ -323,10 +354,8 @@ def tile_gatconv_pa_kernel(tc, X, A, Q, K, Wv, out):
 
         def invert(b, parts):
             row_sums = block[b]["row_sums"]
-            if parts == 2:
-                nc.vector.tensor_tensor(
-                    out=row_sums[:, 0:1], in0=row_sums[:, 0:1], in1=row_sums[:, 1:2], op=ALU.add
-                )
+            if parts > 1:
+                nc.vector.tensor_reduce(out=row_sums[:, 0:1], in_=row_sums[:, :parts], axis=AXIS_X, op=ALU.add)
             inv_sum = codes.tile([P, 1], F32)
             nc.vector.reciprocal(out=inv_sum[:], in_=row_sums[:, 0:1])
             block[b]["inv_sum"] = inv_sum
@@ -354,34 +383,51 @@ def tile_gatconv_pa_kernel(tc, X, A, Q, K, Wv, out):
         first_half, second_half = slice(0, 2), slice(2, N_CHUNKS)
         last = N_BLOCKS - 1
         with tc.manual_schedule():
-            for t0 in range(0, 6, 2):
-                self_products(t0)
-            for t0 in range(0, N_BLOCKS, 4):
-                flip(k_raw, kT, t0)
+            flip(k_raw, kT, 0)
             flip(q_raw, qT, 0)
-            flip(q_raw, qT, 4)
+            first_self_score()
+            self_products(1, 1)
+            self_products(2, 2)
+            flip(k_raw, kT, 4)
+            flip(k_raw, kT, 8)
+            other_scores(0, 0)
+            flip(k_raw, kT, 12)
             group_weights()
             quantise_weights()
-            for g in range(N_PASSES):
-                flip_x(4 * g)
-                flip_x(4 * g + 2)
-                if g < 2:
-                    flip(q_raw, qT, 4 * g + 8)
-                else:
-                    other_scores(0, g - 2)
-                quantise_x(g)
+            flip_x(0)
+            flip_x(2)
+            quantise_x(0)
+            other_scores(0, 1)
+            flip_x(4)
+            flip_x(6)
+            quantise_x(1)
             other_scores(0, 2)
-            self_scores(0)
-            values(0)
             own_mask(0)
-            values(1)
+            flip_x(8)
+            flip_x(10)
+            quantise_x(2)
             own_scores(0)
+            flip_x(12)
+            flip_x(14)
+            values(0)
             for b in range(N_BLOCKS + 1):
                 if b + AHEAD < N_BLOCKS:
                     load_adjacency(b + AHEAD)
                 if b < N_BLOCKS:
-                    mask_others(b)
-                    move_own(b)
+                    new_z(b)
+                    mask_other(b, 0)
+                    if b == 0:
+                        move_own(b)
+                        quantise_x(N_PASSES - 1)
+                    mask_other(b, 1)
+                    mask_other(b, 2)
+                    if b > 0:
+                        move_own(b)
+                if 2 <= b <= N_PASSES:
+                    flip_copy(q_flipped, qT, 4 * b - 4)
+                if b == 0:
+                    values(1)
+                    own_mask(1)
                 if b + 1 < N_BLOCKS:
                     for k in range(OWN):
                         other_scores(b + 1, k)
@@ -389,42 +435,54 @@ def tile_gatconv_pa_kernel(tc, X, A, Q, K, Wv, out):
                             values(k + 2)
                 if 1 <= b < N_BLOCKS:
                     exponentials(b - 1, every, 0)
-                    transposes(b - 1, 0)
-                    transposes(b - 1, 2)
-                if b < 5:
-                    self_products(2 * b + 6)
-                if b + 1 < N_BLOCKS:
+                    transposes(b - 1, first_half)
+                    transposes(b - 1, second_half)
+                if 2 <= b < last:
                     own_mask(b + 1)
+                if b == 0:
+                    self_scores(1, 3)
                 if b in (3, 7, 11):
-                    self_scores(b + 1)
+                    self_scores(b + 1, 4)
                 if 3 <= b < N_BLOCKS:
                     finish(b - 3)
                 if 1 <= b < N_BLOCKS:
-                    regroup(b - 1, 0)
-                    regroup(b - 1, 2)
+                    regroup(b - 1, first_half)
+                    regroup(b - 1, second_half)
+                if b == 1:
+                    own_mask(2)
+                if b < 6:
+                    self_products(2 * b + 4, 2)
                 if b == 1 or b == 2:
                     quantise_values(2 * b - 2)
                     quantise_values(2 * b - 1)
+                if 1 <= b < N_PASSES:
+                    q_flipped = flip_transposes(q_raw, qT, 4 * b)
                 if b == last:
                     minimum(b)
                 if b >= 2:
                     quantise(b - 2, every)
                     invert(b - 2, 1)
+                if 2 <= b < N_BLOCKS:
                     weighted_sum(b - 2)
                 if b + 1 < N_BLOCKS:
                     own_scores(b + 1)
                 if b < last:
                     minimum(b)
             exponentials(last, first_half, 0)
-            exponentials(last, second_half, 1)
-            transposes(last, 0)
-            transposes(last, 2)
-            regroup(last, 0)
-            regroup(last, 2)
+            exponentials(last, slice(2, 3), 1)
+            exponentials(last, slice(3, 4), 2)
+            transposes(last, first_half)
+            transposes(last, slice(2, 3))
             finish(last - 2)
-            finish(last - 1)
+            regroup(last, first_half, nc.vector.tensor_copy)
+            regroup(last, slice(2, 3), nc.vector.tensor_copy)
             quantise(last, first_half)
-            invert(last, 2)
-            quantise(last, second_half)
+            transposes(last, slice(3, 4))
+            weighted_sum(last - 1)
+            regroup(last, slice(3, 4))
+            quantise(last, slice(2, 3))
+            finish(last - 1)
+            invert(last, 3)
+            quantise(last, slice(3, 4))
             weighted_sum(last)
             finish(last)

@@ -108,8 +108,6 @@ def tile_gatconv_pa_kernel(tc, X, A, Q, K, Wv, out):
         load_adjacency(1)
         load_q(4)
         load_adjacency(2)
-        load_q(8)
-        load_q(12)
         load_adjacency(3)
         ident_bf = keep.tile([P, P], BF16)
         make_identity(nc, ident_bf[:])
@@ -171,9 +169,9 @@ def tile_gatconv_pa_kernel(tc, X, A, Q, K, Wv, out):
             dst = flipped[:, :, t0 * P : (t0 + 4) * P]
             src = flip_ps[:].rearrange("p h a j -> p h (a j)")
             if flipped is kT:
-                nc.vector.tensor_copy(out=dst, in_=src)
-            else:
                 nc.vector.tensor_scalar(out=dst, in0=src, scalar1=-1.0, scalar2=None, op0=ALU.mult)
+            else:
+                nc.scalar.copy(out=dst, in_=src)
 
         def flip(raw, flipped, t0):
             flip_copy(flip_transposes(raw, flipped, t0), flipped, t0)
@@ -352,6 +350,12 @@ def tile_gatconv_pa_kernel(tc, X, A, Q, K, Wv, out):
                 in_=block[b]["e_grouped"][:, passes, :, :].rearrange("p g i t -> p (g i t)"),
             )
 
+        def add_sums(b):
+            row_sums = block[b]["row_sums"]
+            nc.gpsimd.tensor_tensor(
+                out=row_sums[:, 0:1], in0=row_sums[:, 0:1], in1=row_sums[:, 1:2], op=ALU.add
+            )
+
         def invert(b, parts):
             row_sums = block[b]["row_sums"]
             if parts > 1:
@@ -379,7 +383,6 @@ def tile_gatconv_pa_kernel(tc, X, A, Q, K, Wv, out):
             nc.scalar.activation(out=o_sb[:], in_=block[b]["o"][:], func=ACT.Copy, scale=block[b]["inv_sum"][:])
             nc.sync.dma_start(out=out[b * P : (b + 1) * P, :], in_=o_sb[:])
 
-        every = slice(0, N_CHUNKS)
         first_half, second_half = slice(0, 2), slice(2, N_CHUNKS)
         last = N_BLOCKS - 1
         with tc.manual_schedule():
@@ -411,6 +414,8 @@ def tile_gatconv_pa_kernel(tc, X, A, Q, K, Wv, out):
             flip_x(14)
             values(0)
             for b in range(N_BLOCKS + 1):
+                if b in (0, 2):
+                    load_q(2 * b + 8)
                 if b + AHEAD < N_BLOCKS:
                     load_adjacency(b + AHEAD)
                 if b < N_BLOCKS:
@@ -421,10 +426,11 @@ def tile_gatconv_pa_kernel(tc, X, A, Q, K, Wv, out):
                         quantise_x(N_PASSES - 1)
                     mask_other(b, 1)
                     mask_other(b, 2)
+                    if b == 1 or b == 2:
+                        quantise_values(2 * b - 2)
+                        quantise_values(2 * b - 1)
                     if b > 0:
                         move_own(b)
-                if 2 <= b <= N_PASSES:
-                    flip_copy(q_flipped, qT, 4 * b - 4)
                 if b == 0:
                     values(1)
                     own_mask(1)
@@ -434,15 +440,15 @@ def tile_gatconv_pa_kernel(tc, X, A, Q, K, Wv, out):
                         if b == 0 and k < 2:
                             values(k + 2)
                 if 1 <= b < N_BLOCKS:
-                    exponentials(b - 1, every, 0)
+                    exponentials(b - 1, first_half, 0)
+                    exponentials(b - 1, second_half, 1)
                     transposes(b - 1, first_half)
                     transposes(b - 1, second_half)
+                    add_sums(b - 1)
                 if 2 <= b < last:
                     own_mask(b + 1)
                 if b == 0:
                     self_scores(1, 3)
-                if b in (3, 7, 11):
-                    self_scores(b + 1, 4)
                 if 3 <= b < N_BLOCKS:
                     finish(b - 3)
                 if 1 <= b < N_BLOCKS:
@@ -450,22 +456,23 @@ def tile_gatconv_pa_kernel(tc, X, A, Q, K, Wv, out):
                     regroup(b - 1, second_half)
                 if b == 1:
                     own_mask(2)
-                if b < 6:
-                    self_products(2 * b + 4, 2)
-                if b == 1 or b == 2:
-                    quantise_values(2 * b - 2)
-                    quantise_values(2 * b - 1)
-                if 1 <= b < N_PASSES:
-                    q_flipped = flip_transposes(q_raw, qT, 4 * b)
+                if 1 <= b < 7:
+                    self_products(2 * b + 2, 2)
+                if b in (2, 5, 8):
+                    flip_copy(q_flipped, qT, 4 * (b // 3) + 4)
                 if b == last:
                     minimum(b)
+                if 3 <= b < 9:
+                    self_scores(2 * b - 2, 2)
                 if b >= 2:
-                    quantise(b - 2, every)
+                    quantise(b - 2, slice(0, N_PASSES))
                     invert(b - 2, 1)
                 if 2 <= b < N_BLOCKS:
                     weighted_sum(b - 2)
                 if b + 1 < N_BLOCKS:
                     own_scores(b + 1)
+                if b in (1, 4, 7):
+                    q_flipped = flip_transposes(q_raw, qT, 4 * (b // 3) + 4)
                 if b < last:
                     minimum(b)
             exponentials(last, first_half, 0)

@@ -46,7 +46,7 @@ def tile_gatconv_pa_kernel(tc, X, A, Q, K, Wv, out):
         keep = stack.enter_context(tc.tile_pool(name="keep", bufs=1))
         stage = stack.enter_context(tc.tile_pool(name="stage", bufs=3))
         codes = stack.enter_context(tc.tile_pool(name="codes", bufs=5))
-        zs = stack.enter_context(tc.tile_pool(name="zs", bufs=2))
+        zs = stack.enter_context(tc.tile_pool(name="zs", bufs=3))
         stats = stack.enter_context(tc.tile_pool(name="stats", bufs=4))
         adjacency = stack.enter_context(tc.tile_pool(name="adjacency", bufs=4))
         psum_s = stack.enter_context(tc.psum_pool(name="psum_s", bufs=4))
@@ -56,16 +56,22 @@ def tile_gatconv_pa_kernel(tc, X, A, Q, K, Wv, out):
         k_raw = keep.tile([P, N_BLOCKS, D_HID], BF16)
         q_raw = keep.tile([P, N_BLOCKS, D_HID], BF16)
         x_raw = keep.tile([P, N_BLOCKS, D_IN], BF16)
-        k_view = K.rearrange("(t p) h -> p t h", p=P)
-        q_view = Q.rearrange("(t p) h -> p t h", p=P)
+        k_view = K.rearrange("(c p r) h -> p c (r h)", p=P, r=4)
+        q_view = Q.rearrange("(c p r) h -> p c (r h)", p=P, r=4)
+        a_view = A.bitcast(I32).rearrange("(c p r) w -> p c r w", p=P, r=4)
+        out_view = out.rearrange("(c p r) d -> p c r d", p=P, r=4)
         x_view = X.rearrange("(v p r) f -> p v (r f)", p=P, r=2)
         wv_raw = keep.tile([P, PACK, D_OUT], BF16)
 
         def load_k(t0):
-            nc.sync.dma_start(out=k_raw[:, t0 : t0 + 4, :], in_=k_view[:, t0 : t0 + 4, :])
+            nc.sync.dma_start(
+                out=k_raw[:, t0 : t0 + 4, :].rearrange("p r h -> p (r h)"), in_=k_view[:, t0 // 4, :]
+            )
 
         def load_q(t0):
-            nc.sync.dma_start(out=q_raw[:, t0 : t0 + 4, :], in_=q_view[:, t0 : t0 + 4, :])
+            nc.sync.dma_start(
+                out=q_raw[:, t0 : t0 + 4, :].rearrange("p r h -> p (r h)"), in_=q_view[:, t0 // 4, :]
+            )
 
         def load_x(t0):
             nc.sync.dma_start(
@@ -92,7 +98,7 @@ def tile_gatconv_pa_kernel(tc, X, A, Q, K, Wv, out):
             for cols in pieces:
                 nc.sync.dma_start(
                     out=a_blk[:, cols, :].rearrange("p j w -> p (j w)"),
-                    in_=A.bitcast(I32)[b * P : (b + 1) * P, 2 * cols.start : 2 * cols.stop],
+                    in_=a_view[:, b // 4, b % 4, 2 * cols.start : 2 * cols.stop],
                 )
             block[b]["edges"] = a_blk[:, :, 0]
             block[b]["edges_u32"] = a_blk[:].bitcast(U32)[:, :, 0]
@@ -156,7 +162,12 @@ def tile_gatconv_pa_kernel(tc, X, A, Q, K, Wv, out):
         kT = keep.tile([P, H_HALVES, N_NODES], BF16)
         qT = keep.tile([P, H_HALVES, N_NODES], BF16)
         def flip_transposes(raw, flipped, t0):
-            pool, tag = (psum_t, "t") if flipped is kT else (psum_o, "o")
+            if flipped is qT:
+                pool, tag = psum_o, "o"
+            elif t0 == 8:
+                pool, tag = psum_s, "s"
+            else:
+                pool, tag = psum_t, "t"
             flip_ps = pool.tile([P, H_HALVES, 4, P], BF16, tag=tag)
             for half in range(H_HALVES):
                 for a in range(4):
@@ -167,11 +178,14 @@ def tile_gatconv_pa_kernel(tc, X, A, Q, K, Wv, out):
 
         def flip_copy(flip_ps, flipped, t0):
             dst = flipped[:, :, t0 * P : (t0 + 4) * P]
-            src = flip_ps[:].rearrange("p h a j -> p h (a j)")
             if flipped is kT:
+                nc.scalar.copy(out=dst.rearrange("p h (j r) -> p h j r", r=4), in_=flip_ps[:].rearrange("p h r j -> p h j r"))
+                return
+            src = flip_ps[:].rearrange("p h r j -> p h (r j)")
+            if t0 == 0:
                 nc.vector.tensor_scalar(out=dst, in0=src, scalar1=-1.0, scalar2=None, op0=ALU.mult)
             else:
-                nc.scalar.copy(out=dst, in_=src)
+                nc.scalar.activation(out=dst, in_=src, func=ACT.Copy, scale=-1.0)
 
         def flip(raw, flipped, t0):
             flip_copy(flip_transposes(raw, flipped, t0), flipped, t0)
@@ -242,8 +256,7 @@ def tile_gatconv_pa_kernel(tc, X, A, Q, K, Wv, out):
             cols = slice(own_chunk * BANK, (own_chunk + 1) * BANK)
             mask = stage.tile([P, BANK], BF16)
             nc.scalar.activation(out=mask[:], in_=block[b]["edges_u32"][:, cols], func=ACT.Copy, scale=-1.0, bias=1.0)
-            first = b * P - own_chunk * BANK
-            own = mask[:, first : first + P]
+            own = mask[:, b % 4 :: 4]
             nc.gpsimd.tensor_tensor(out=own, in0=own, in1=off_diagonal[:], op=ALU.mult)
             block[b]["mask"] = mask
 
@@ -381,7 +394,7 @@ def tile_gatconv_pa_kernel(tc, X, A, Q, K, Wv, out):
         def finish(b):
             o_sb = stage.tile([P, D_OUT], F32)
             nc.scalar.activation(out=o_sb[:], in_=block[b]["o"][:], func=ACT.Copy, scale=block[b]["inv_sum"][:])
-            nc.sync.dma_start(out=out[b * P : (b + 1) * P, :], in_=o_sb[:])
+            nc.sync.dma_start(out=out_view[:, b // 4, b % 4, :], in_=o_sb[:])
 
         first_half, second_half = slice(0, 2), slice(2, N_CHUNKS)
         last = N_BLOCKS - 1
@@ -393,59 +406,63 @@ def tile_gatconv_pa_kernel(tc, X, A, Q, K, Wv, out):
             self_products(2, 2)
             flip(k_raw, kT, 4)
             flip(k_raw, kT, 8)
-            other_scores(0, 0)
             flip(k_raw, kT, 12)
+            new_z(0)
+            other_scores(0, 0)
             group_weights()
             quantise_weights()
             flip_x(0)
             flip_x(2)
-            quantise_x(0)
             other_scores(0, 1)
+            quantise_x(0)
             flip_x(4)
             flip_x(6)
-            quantise_x(1)
+            mask_other(0, 0)
             other_scores(0, 2)
+            quantise_x(1)
             own_mask(0)
             flip_x(8)
             flip_x(10)
-            quantise_x(2)
+            mask_other(0, 1)
             own_scores(0)
+            quantise_x(2)
             flip_x(12)
             flip_x(14)
+            mask_other(0, 2)
+            move_own(0)
+            own_mask(1)
             values(0)
+            quantise_x(3)
             for b in range(N_BLOCKS + 1):
                 if b in (0, 2):
                     load_q(2 * b + 8)
                 if b + AHEAD < N_BLOCKS:
                     load_adjacency(b + AHEAD)
                 if b < N_BLOCKS:
-                    new_z(b)
-                    mask_other(b, 0)
-                    if b == 0:
-                        move_own(b)
-                        quantise_x(N_PASSES - 1)
-                    mask_other(b, 1)
-                    mask_other(b, 2)
+                    if b > 0:
+                        new_z(b)
+                        for k in range(OWN):
+                            mask_other(b, k)
                     if b == 1 or b == 2:
                         quantise_values(2 * b - 2)
                         quantise_values(2 * b - 1)
                     if b > 0:
                         move_own(b)
-                if b == 0:
-                    values(1)
-                    own_mask(1)
                 if b + 1 < N_BLOCKS:
                     for k in range(OWN):
                         other_scores(b + 1, k)
-                        if b == 0 and k < 2:
-                            values(k + 2)
+                if b == 0:
+                    values(1)
+                    own_scores(1)
+                    values(2)
+                    values(3)
                 if 1 <= b < N_BLOCKS:
                     exponentials(b - 1, first_half, 0)
                     exponentials(b - 1, second_half, 1)
                     transposes(b - 1, first_half)
                     transposes(b - 1, second_half)
                     add_sums(b - 1)
-                if 2 <= b < last:
+                if 1 <= b < last:
                     own_mask(b + 1)
                 if b == 0:
                     self_scores(1, 3)
@@ -454,8 +471,6 @@ def tile_gatconv_pa_kernel(tc, X, A, Q, K, Wv, out):
                 if 1 <= b < N_BLOCKS:
                     regroup(b - 1, first_half)
                     regroup(b - 1, second_half)
-                if b == 1:
-                    own_mask(2)
                 if 1 <= b < 7:
                     self_products(2 * b + 2, 2)
                 if b in (2, 5, 8):
@@ -469,7 +484,7 @@ def tile_gatconv_pa_kernel(tc, X, A, Q, K, Wv, out):
                     invert(b - 2, 1)
                 if 2 <= b < N_BLOCKS:
                     weighted_sum(b - 2)
-                if b + 1 < N_BLOCKS:
+                if 0 < b < last:
                     own_scores(b + 1)
                 if b in (1, 4, 7):
                     q_flipped = flip_transposes(q_raw, qT, 4 * (b // 3) + 4)

@@ -333,9 +333,9 @@ def tile_gatconv_pa_kernel(tc, X, A, Q, K, Wv, out):
                 accum_out=block[b]["row_sums"][:, part : part + 1],
             )
 
-        def transposes(b, slots):
+        def transposes(b, slots, pool=psum_t, tag="t"):
             e_words = block[b]["e"][:].bitcast(F32)
-            et_ps = psum_t.tile([P, 2, 2, P], F32, tag="t")
+            et_ps = pool.tile([P, 2, 2, P], F32, tag=tag)
             for a, slot in enumerate(range(slots.start, slots.stop)):
                 for u in range(2):
                     nc.tensor.transpose(et_ps[:, a, u, :], e_words[:, slot, u * P : (u + 1) * P], ident_f32[:])
@@ -449,8 +449,10 @@ def tile_gatconv_pa_kernel(tc, X, A, Q, K, Wv, out):
                     if b > 0:
                         move_own(b)
                 if b + 1 < N_BLOCKS:
-                    for k in range(OWN):
-                        other_scores(b + 1, k)
+                    other_scores(b + 1, 0)
+                    other_scores(b + 1, 1)
+                if b == 0:
+                    other_scores(b + 1, 2)
                 if b == 0:
                     values(1)
                     own_scores(1)
@@ -460,6 +462,8 @@ def tile_gatconv_pa_kernel(tc, X, A, Q, K, Wv, out):
                     exponentials(b - 1, first_half, 0)
                     exponentials(b - 1, second_half, 1)
                     transposes(b - 1, first_half)
+                    if b < last:
+                        other_scores(b + 1, 2)
                     transposes(b - 1, second_half)
                     add_sums(b - 1)
                 if 1 <= b < last:
@@ -475,8 +479,6 @@ def tile_gatconv_pa_kernel(tc, X, A, Q, K, Wv, out):
                     self_products(2 * b + 2, 2)
                 if b in (2, 5, 8):
                     flip_copy(q_flipped, qT, 4 * (b // 3) + 4)
-                if b == last:
-                    minimum(b)
                 if 3 <= b < 9:
                     self_scores(2 * b - 2, 2)
                 if b >= 2:
@@ -488,18 +490,18 @@ def tile_gatconv_pa_kernel(tc, X, A, Q, K, Wv, out):
                     own_scores(b + 1)
                 if b in (1, 4, 7):
                     q_flipped = flip_transposes(q_raw, qT, 4 * (b // 3) + 4)
-                if b < last:
+                if b < N_BLOCKS:
                     minimum(b)
             exponentials(last, first_half, 0)
             exponentials(last, slice(2, 3), 1)
             exponentials(last, slice(3, 4), 2)
             transposes(last, first_half)
-            transposes(last, slice(2, 3))
+            transposes(last, slice(2, 3), psum_s, "s")
+            transposes(last, slice(3, 4), psum_s, "s")
             finish(last - 2)
             regroup(last, first_half, nc.vector.tensor_copy)
             regroup(last, slice(2, 3), nc.vector.tensor_copy)
             quantise(last, first_half)
-            transposes(last, slice(3, 4))
             weighted_sum(last - 1)
             regroup(last, slice(3, 4))
             quantise(last, slice(2, 3))

@@ -46,6 +46,7 @@ def tile_gatconv_pa_kernel(tc, X, A, Q, K, Wv, out):
         keep = stack.enter_context(tc.tile_pool(name="keep", bufs=1))
         stage = stack.enter_context(tc.tile_pool(name="stage", bufs=3))
         codes = stack.enter_context(tc.tile_pool(name="codes", bufs=5))
+        results = stack.enter_context(tc.tile_pool(name="results", bufs=N_BLOCKS))
         zs = stack.enter_context(tc.tile_pool(name="zs", bufs=3))
         stats = stack.enter_context(tc.tile_pool(name="stats", bufs=4))
         adjacency = stack.enter_context(tc.tile_pool(name="adjacency", bufs=4))
@@ -55,7 +56,7 @@ def tile_gatconv_pa_kernel(tc, X, A, Q, K, Wv, out):
 
         k_raw = keep.tile([P, N_BLOCKS, D_HID], BF16)
         q_raw = keep.tile([P, N_BLOCKS, D_HID], BF16)
-        x_raw = keep.tile([P, N_BLOCKS, D_IN], BF16)
+        x_raw = adjacency.tile([P, N_BLOCKS, D_IN], BF16, tag="a")
         k_view = K.rearrange("(c p r) h -> p c (r h)", p=P, r=4)
         q_view = Q.rearrange("(c p r) h -> p c (r h)", p=P, r=4)
         a_view = A.bitcast(I32).rearrange("(c p r) w -> p c r w", p=P, r=4)
@@ -92,7 +93,7 @@ def tile_gatconv_pa_kernel(tc, X, A, Q, K, Wv, out):
             block[b]["chunks"] = [c for c in range(N_CHUNKS) if c != own_chunk] + [own_chunk]
 
         def load_adjacency(b):
-            a_blk = adjacency.tile([P, N_NODES, 2], I32)
+            a_blk = adjacency.tile([P, N_NODES, 2], I32, tag="a")
             order = block[b]["chunks"][OWN:] + block[b]["chunks"][:OWN]
             pieces = [slice(c * BANK, (c + 1) * BANK) for c in order] if b < 2 else [slice(0, N_NODES)]
             for cols in pieces:
@@ -122,10 +123,6 @@ def tile_gatconv_pa_kernel(tc, X, A, Q, K, Wv, out):
         no_edge_ident = keep.tile([P, P], BF16)
         nc.vector.tensor_scalar(
             out=no_edge_ident[:], in0=ident_bf[:], scalar1=NO_EDGE, scalar2=None, op0=ALU.mult
-        )
-        minus_ident = keep.tile([P, P], BF16)
-        nc.vector.tensor_scalar(
-            out=minus_ident[:], in0=ident_bf[:], scalar1=-1.0, scalar2=None, op0=ALU.mult
         )
         off_diagonal = keep.tile([P, P], BF16)
         nc.vector.tensor_scalar(
@@ -392,9 +389,12 @@ def tile_gatconv_pa_kernel(tc, X, A, Q, K, Wv, out):
             block[b]["o"] = o_ps
 
         def finish(b):
-            o_sb = stage.tile([P, D_OUT], F32)
+            o_sb = results.tile([P, D_OUT], F32)
             nc.scalar.activation(out=o_sb[:], in_=block[b]["o"][:], func=ACT.Copy, scale=block[b]["inv_sum"][:])
-            nc.sync.dma_start(out=out_view[:, b // 4, b % 4, :], in_=o_sb[:])
+            block[b]["result"] = o_sb
+
+        def store(b):
+            nc.sync.dma_start(out=out_view[:, b // 4, b % 4, :], in_=block[b]["result"][:])
 
         first_half, second_half = slice(0, 2), slice(2, N_CHUNKS)
         last = N_BLOCKS - 1
@@ -472,6 +472,11 @@ def tile_gatconv_pa_kernel(tc, X, A, Q, K, Wv, out):
                     self_scores(1, 3)
                 if 3 <= b < N_BLOCKS:
                     finish(b - 3)
+                if b == N_BLOCKS - AHEAD:
+                    for done in range(b - 2):
+                        store(done)
+                if N_BLOCKS - AHEAD < b < N_BLOCKS:
+                    store(b - 3)
                 if 1 <= b < N_BLOCKS:
                     regroup(b - 1, first_half)
                     regroup(b - 1, second_half)
@@ -499,6 +504,7 @@ def tile_gatconv_pa_kernel(tc, X, A, Q, K, Wv, out):
             transposes(last, slice(2, 3), psum_s, "s")
             transposes(last, slice(3, 4), psum_s, "s")
             finish(last - 2)
+            store(last - 2)
             regroup(last, first_half, nc.vector.tensor_copy)
             regroup(last, slice(2, 3), nc.vector.tensor_copy)
             quantise(last, first_half)
@@ -506,7 +512,9 @@ def tile_gatconv_pa_kernel(tc, X, A, Q, K, Wv, out):
             regroup(last, slice(3, 4))
             quantise(last, slice(2, 3))
             finish(last - 1)
+            store(last - 1)
             invert(last, 3)
             quantise(last, slice(3, 4))
             weighted_sum(last)
             finish(last)
+            store(last)

from contextlib import ExitStack

import concourse.mybir as mybir
from concourse.masks import make_identity

F32 = mybir.dt.float32
BF16 = mybir.dt.bfloat16
I32 = mybir.dt.int32
U32 = mybir.dt.uint32
U8 = mybir.dt.uint8
FP8X4 = mybir.dt.float8_e4m3fn_x4
ALU = mybir.AluOpType
ACT = mybir.ActivationFunctionType
AXIS_X = mybir.AxisListType.X

P = 128
PACK = 4
K_PASS = P * PACK
BANK = 512

N_NODES = 2048
D_IN = 512
D_HID = 256
D_OUT = 256

N_BLOCKS = N_NODES // P
N_PASSES = N_NODES // K_PASS
N_CHUNKS = N_NODES // BANK
H_HALVES = D_HID // P

NO_EDGE = 2.0**126

SELF_SCORE = 48.0

OWN = N_CHUNKS - 1
Z_FIRST = 4

AHEAD = 4

FLOPS = 2 * N_NODES * (D_IN * D_OUT + N_NODES * D_HID + N_NODES * D_OUT)


def tile_gatconv_pa_kernel(tc, X, A, Q, K, Wv, out):
    nc = tc.nc
    with ExitStack() as stack:
        keep = stack.enter_context(tc.tile_pool(name="keep", bufs=1))
        stage = stack.enter_context(tc.tile_pool(name="stage", bufs=3))
        codes = stack.enter_context(tc.tile_pool(name="codes", bufs=5))
        results = stack.enter_context(tc.tile_pool(name="results", bufs=N_BLOCKS))
        zs = stack.enter_context(tc.tile_pool(name="zs", bufs=3))
        stats = stack.enter_context(tc.tile_pool(name="stats", bufs=4))
        adjacency = stack.enter_context(tc.tile_pool(name="adjacency", bufs=4))
        psum_s = stack.enter_context(tc.psum_pool(name="psum_s", bufs=4))
        psum_t = stack.enter_context(tc.psum_pool(name="psum_t", bufs=2))
        psum_o = stack.enter_context(tc.psum_pool(name="psum_o", bufs=2))

        k_raw = keep.tile([P, N_BLOCKS, D_HID], BF16)
        q_raw = keep.tile([P, N_BLOCKS, D_HID], BF16)
        x_raw = adjacency.tile([P, N_BLOCKS, D_IN], BF16, tag="a")
        k_view = K.rearrange("(c p r) h -> p c (r h)", p=P, r=4)
        q_view = Q.rearrange("(c p r) h -> p c (r h)", p=P, r=4)
        a_view = A.bitcast(I32).rearrange("(c p r) w -> p c r w", p=P, r=4)
        out_view = out.rearrange("(c p r) d -> p c r d", p=P, r=4)
        x_view = X.rearrange("(v p r) f -> p v (r f)", p=P, r=2)
        wv_raw = keep.tile([P, PACK, D_OUT], BF16)

        def load_k(t0):
            nc.sync.dma_start(
                out=k_raw[:, t0 : t0 + 4, :].rearrange("p r h -> p (r h)"), in_=k_view[:, t0 // 4, :]
            )

        def load_q(t0):
            nc.sync.dma_start(
                out=q_raw[:, t0 : t0 + 4, :].rearrange("p r h -> p (r h)"), in_=q_view[:, t0 // 4, :]
            )

        def load_x(t0):
            nc.sync.dma_start(
                out=x_raw[:, t0 : t0 + 4, :].rearrange("p (v r) f -> p v (r f)", r=2),
                in_=x_view[:, t0 // 2 : t0 // 2 + 2, :],
            )

        def load_weights():
            nc.sync.dma_start(
                out=wv_raw[:].rearrange("p (u e) n -> p u (e n)", u=2),
                in_=Wv.rearrange("(u p e) n -> p u (e n)", u=2, p=P, e=2),
            )

        block = {b: {} for b in range(N_BLOCKS)}

        for b in range(N_BLOCKS):
            own_chunk = b // (N_BLOCKS // N_CHUNKS)
            block[b]["chunks"] = [c for c in range(N_CHUNKS) if c != own_chunk] + [own_chunk]

        def load_adjacency(b):
            a_blk = adjacency.tile([P, N_NODES, 2], I32, tag="a")
            order = block[b]["chunks"][OWN:] + block[b]["chunks"][:OWN]
            pieces = [slice(c * BANK, (c + 1) * BANK) for c in order] if b < 2 else [slice(0, N_NODES)]
            for cols in pieces:
                nc.sync.dma_start(
                    out=a_blk[:, cols, :].rearrange("p j w -> p (j w)"),
                    in_=a_view[:, b // 4, b % 4, 2 * cols.start : 2 * cols.stop],
                )
            block[b]["edges"] = a_blk[:, :, 0]
            block[b]["edges_u32"] = a_blk[:].bitcast(U32)[:, :, 0]

        load_k(0)
        load_q(0)
        for t0 in range(4, N_BLOCKS, 4):
            load_k(t0)
        load_weights()
        for t0 in range(0, N_BLOCKS, 4):
            load_x(t0)
        load_adjacency(0)
        load_adjacency(1)
        load_q(4)
        load_adjacency(2)
        load_adjacency(3)
        ident_bf = keep.tile([P, P], BF16)
        make_identity(nc, ident_bf[:])
        ident_f32 = keep.tile([P, P], F32)
        make_identity(nc, ident_f32[:])
        no_edge_ident = keep.tile([P, P], BF16)
        nc.vector.tensor_scalar(
            out=no_edge_ident[:], in0=ident_bf[:], scalar1=NO_EDGE, scalar2=None, op0=ALU.mult
        )
        off_diagonal = keep.tile([P, P], BF16)
        nc.vector.tensor_scalar(
            out=off_diagonal[:], in0=ident_bf[:], scalar1=-1.0, scalar2=1.0, op0=ALU.mult, op1=ALU.add
        )

        shifts = keep.tile([P, N_BLOCKS], F32)
        folded = keep.tile([P, N_BLOCKS, 33], F32)
        nc.gpsimd.memset(folded[:, :, 32:33], -SELF_SCORE)

        def self_products(t0, n):
            products = stage.tile([P, 2, D_HID], F32)
            tiles = slice(t0, t0 + n)
            nc.gpsimd.tensor_tensor(
                out=products[:, :n, :], in0=q_raw[:, tiles, :], in1=k_raw[:, tiles, :], op=ALU.mult
            )
            for width in (128, 64, 32):
                dst = products[:, :n, :width] if width > 32 else folded[:, tiles, :32]
                nc.gpsimd.tensor_tensor(
                    out=dst, in0=products[:, :n, :width], in1=products[:, :n, width : 2 * width], op=ALU.add
                )

        def self_scores(t0, n):
            nc.vector.tensor_reduce(
                out=shifts[:, t0 : t0 + n], in_=folded[:, t0 : t0 + n, :], axis=AXIS_X, op=ALU.add
            )

        def first_self_score():
            products = keep.tile([P, D_HID + 1], F32)
            nc.vector.memset(products[:, D_HID:], -SELF_SCORE)
            nc.vector.tensor_tensor(out=products[:, :D_HID], in0=q_raw[:, 0, :], in1=k_raw[:, 0, :], op=ALU.mult)
            nc.vector.tensor_reduce(out=shifts[:, 0:1], in_=products[:], axis=AXIS_X, op=ALU.add)

        kT = keep.tile([P, H_HALVES, N_NODES], BF16)
        qT = keep.tile([P, H_HALVES, N_NODES], BF16)
        def flip_transposes(raw, flipped, t0):
            if flipped is qT:
                pool, tag = psum_o, "o"
            elif t0 == 8:
                pool, tag = psum_s, "s"
            else:
                pool, tag = psum_t, "t"
            flip_ps = pool.tile([P, H_HALVES, 4, P], BF16, tag=tag)
            for half in range(H_HALVES):
                for a in range(4):
                    nc.tensor.transpose(
                        flip_ps[:, half, a, :], raw[:, t0 + a, half * P : (half + 1) * P], ident_bf[:]
                    )
            return flip_ps

        def flip_copy(flip_ps, flipped, t0):
            dst = flipped[:, :, t0 * P : (t0 + 4) * P]
            if flipped is kT:
                nc.scalar.copy(out=dst.rearrange("p h (j r) -> p h j r", r=4), in_=flip_ps[:].rearrange("p h r j -> p h j r"))
                return
            src = flip_ps[:].rearrange("p h r j -> p h (r j)")
            if t0 == 0:
                nc.vector.tensor_scalar(out=dst, in0=src, scalar1=-1.0, scalar2=None, op0=ALU.mult)
            else:
                nc.scalar.activation(out=dst, in_=src, func=ACT.Copy, scale=-1.0)

        def flip(raw, flipped, t0):
            flip_copy(flip_transposes(raw, flipped, t0), flipped, t0)

        wv_grouped = keep.tile([P, D_OUT, PACK], BF16, align_bytes=64)

        def group_weights():
            nc.vector.tensor_copy(out=wv_grouped[:], in_=wv_raw[:].rearrange("p t n -> p n t"))

        wv_codes = keep.tile([P, D_OUT], U32, align_bytes=64)
        wv_scales = keep.tile([P, D_OUT], U8, align_bytes=64)

        x_words = x_raw[:].bitcast(F32)
        x_grouped = keep.tile([P, N_BLOCKS, P, PACK], BF16, align_bytes=64)
        x_grouped_words = x_grouped[:].bitcast(F32)
        x_codes = keep.tile([P, N_BLOCKS, P], U32, align_bytes=64)
        x_scales = keep.tile([P, N_BLOCKS, P], U8, align_bytes=64)
        v_grouped = keep.tile([P, N_PASSES, D_OUT, PACK], BF16, align_bytes=64)
        v_codes = keep.tile([P, N_PASSES, D_OUT], U32, align_bytes=64)
        v_scales = keep.tile([P, N_PASSES, D_OUT], U8, align_bytes=64)
        def flip_x(t0):
            xt_ps = psum_t.tile([P, 2, 2, P], F32, tag="t")
            for a in range(2):
                for u in range(2):
                    nc.tensor.transpose(xt_ps[:, a, u, :], x_words[:, t0 + a, u * P : (u + 1) * P], ident_f32[:])
            nc.scalar.copy(out=x_grouped_words[:, t0 : t0 + 2, :, :], in_=xt_ps[:].rearrange("p a u r -> p a r u"))

        def quantise_weights():
            nc.vector.quantize_mx(
                out=wv_codes[:].bitcast(FP8X4),
                scales=wv_scales[:],
                in_=wv_grouped[:].rearrange("p n t -> p (n t)"),
            )

        def quantise_x(g):
            tiles = slice(g * PACK, (g + 1) * PACK)
            nc.vector.quantize_mx(
                out=x_codes[:, tiles, :].rearrange("p t r -> p (t r)").bitcast(FP8X4),
                scales=x_scales[:, tiles, :].rearrange("p t r -> p (t r)"),
                in_=x_grouped[:, tiles, :, :].rearrange("p t r k -> p (t r k)"),
            )

        def values(g):
            for half in range(D_OUT // P):
                cols = slice(half * P, (half + 1) * P)
                v_ps = psum_o.tile([P, PACK, P], F32, tag="o")
                for t in range(PACK):
                    nc.tensor.matmul_mx(
                        out=v_ps[:, t, :],
                        lhsT=x_codes[:, g * PACK + t, :].bitcast(FP8X4),
                        lhsT_scale=x_scales[:, g * PACK + t, :],
                        rhs=wv_codes[:, cols].bitcast(FP8X4),
                        rhs_scale=wv_scales[:, cols],
                        start=True,
                        stop=True,
                    )
                nc.scalar.copy(out=v_grouped[:, g, cols, :], in_=v_ps[:].rearrange("p t d -> p d t"))

        def quantise_values(g):
            nc.vector.quantize_mx(
                out=v_codes[:, g, :].bitcast(FP8X4),
                scales=v_scales[:, g, :],
                in_=v_grouped[:, g, :, :].rearrange("p d t -> p (d t)"),
            )

        def own_mask(b):
            own_chunk = block[b]["chunks"][OWN]
            cols = slice(own_chunk * BANK, (own_chunk + 1) * BANK)
            mask = stage.tile([P, BANK], BF16)
            nc.scalar.activation(out=mask[:], in_=block[b]["edges_u32"][:, cols], func=ACT.Copy, scale=-1.0, bias=1.0)
            own = mask[:, b % 4 :: 4]
            nc.gpsimd.tensor_tensor(out=own, in0=own, in1=off_diagonal[:], op=ALU.mult)
            block[b]["mask"] = mask

        def score_matmuls(b, chunk, own):
            s_ps = psum_s.tile([P, BANK], F32, tag="s")
            for half in range(H_HALVES):
                nc.tensor.matmul(
                    out=s_ps[:],
                    lhsT=qT[:, half, b * P : (b + 1) * P],
                    rhs=kT[:, half, chunk * BANK : (chunk + 1) * BANK],
                    start=(half == 0),
                    stop=(half == H_HALVES - 1 and not own),
                )
            if own:
                nc.tensor.matmul(
                    out=s_ps[:], lhsT=no_edge_ident[:], rhs=block[b]["mask"][:], start=False, stop=True
                )
            return s_ps

        def other_scores(b, k):
            block[b]["s", k] = score_matmuls(b, block[b]["chunks"][k], own=False)

        def own_scores(b):
            block[b]["s", OWN] = score_matmuls(b, block[b]["chunks"][OWN], own=True)

        def new_z(b):
            z = zs.tile([P, Z_FIRST + N_NODES], F32)
            block[b]["z"] = z

        def mask_other(b, k):
            c = block[b]["chunks"][k]
            nc.vector.scalar_tensor_tensor(
                out=block[b]["z"][:, Z_FIRST + k * BANK : Z_FIRST + (k + 1) * BANK],
                in0=block[b]["s", k][:],
                scalar=shifts[:, b : b + 1],
                in1=block[b]["edges"][:, c * BANK : (c + 1) * BANK],
                op0=ALU.add,
                op1=ALU.mult,
            )

        def move_own(b):
            nc.vector.tensor_scalar(
                out=block[b]["z"][:, Z_FIRST + OWN * BANK :],
                in0=block[b]["s", OWN][:],
                scalar1=shifts[:, b : b + 1],
                scalar2=None,
                op0=ALU.add,
                op1=ALU.min,
                accum_out=block[b]["z"][:, Z_FIRST - 1 : Z_FIRST],
            )

        def minimum(b):
            row_min = stats.tile([P, 1], F32)
            nc.vector.tensor_reduce(
                out=row_min[:],
                in_=block[b]["z"][:, Z_FIRST - 1 : Z_FIRST + OWN * BANK],
                axis=AXIS_X,
                op=ALU.min,
            )
            block[b]["row_min"] = row_min

        def exponentials(b, slots, part):
            if part == 0:
                e_blk = stage.tile([P, N_CHUNKS, BANK], BF16)
                row_sums = stats.tile([P, 3], F32)
                block[b]["e"] = e_blk
                block[b]["row_sums"] = row_sums
            nc.scalar.activation(
                out=block[b]["e"][:, slots, :].rearrange("p c j -> p (c j)"),
                in_=block[b]["z"][:, Z_FIRST + slots.start * BANK : Z_FIRST + slots.stop * BANK],
                func=ACT.Exp,
                bias=block[b]["row_min"][:],
                scale=-1.0,
                accum_out=block[b]["row_sums"][:, part : part + 1],
            )

        def transposes(b, slots, pool=psum_t, tag="t"):
            e_words = block[b]["e"][:].bitcast(F32)
            et_ps = pool.tile([P, 2, 2, P], F32, tag=tag)
            for a, slot in enumerate(range(slots.start, slots.stop)):
                for u in range(2):
                    nc.tensor.transpose(et_ps[:, a, u, :], e_words[:, slot, u * P : (u + 1) * P], ident_f32[:])
            block[b]["eT", slots.start] = et_ps

        def regroup(b, slots, copy=nc.scalar.copy):
            if slots.start == 0:
                e_grouped = stage.tile([P, N_PASSES, P, PACK], BF16, align_bytes=64)
                block[b]["e_grouped"] = e_grouped
            e_grouped_words = block[b]["e_grouped"][:].bitcast(F32)
            copy(
                out=e_grouped_words[:, slots, :, :],
                in_=block[b]["eT", slots.start][:, : slots.stop - slots.start, :, :].rearrange("p a u i -> p a i u"),
            )

        def quantise(b, passes):
            if passes.start == 0:
                e_codes = codes.tile([P, N_PASSES, P], U32, align_bytes=64)
                e_scales = codes.tile([P, N_PASSES, P], U8, align_bytes=64)
                block[b]["e_codes"] = e_codes
                block[b]["e_scales"] = e_scales
            nc.vector.quantize_mx(
                out=block[b]["e_codes"][:, passes, :].rearrange("p g i -> p (g i)").bitcast(FP8X4),
                scales=block[b]["e_scales"][:, passes, :].rearrange("p g i -> p (g i)"),
                in_=block[b]["e_grouped"][:, passes, :, :].rearrange("p g i t -> p (g i t)"),
            )

        def add_sums(b):
            row_sums = block[b]["row_sums"]
            nc.gpsimd.tensor_tensor(
                out=row_sums[:, 0:1], in0=row_sums[:, 0:1], in1=row_sums[:, 1:2], op=ALU.add
            )

        def invert(b, parts):
            row_sums = block[b]["row_sums"]
            if parts > 1:
                nc.vector.tensor_reduce(out=row_sums[:, 0:1], in_=row_sums[:, :parts], axis=AXIS_X, op=ALU.add)
            inv_sum = codes.tile([P, 1], F32)
            nc.vector.reciprocal(out=inv_sum[:], in_=row_sums[:, 0:1])
            block[b]["inv_sum"] = inv_sum

        def weighted_sum(b):
            o_ps = psum_o.tile([P, D_OUT], F32, tag="o")
            for g in range(N_PASSES):
                nc.tensor.matmul_mx(
                    out=o_ps[:],
                    lhsT=block[b]["e_codes"][:, g, :].bitcast(FP8X4),
                    lhsT_scale=block[b]["e_scales"][:, g, :],
                    rhs=v_codes[:, block[b]["chunks"][g], :].bitcast(FP8X4),
                    rhs_scale=v_scales[:, block[b]["chunks"][g], :],
                    start=(g == 0),
                    stop=(g == N_PASSES - 1),
                )
            block[b]["o"] = o_ps

        def finish(b):
            o_sb = results.tile([P, D_OUT], F32)
            nc.scalar.activation(out=o_sb[:], in_=block[b]["o"][:], func=ACT.Copy, scale=block[b]["inv_sum"][:])
            block[b]["result"] = o_sb

        def store(b):
            nc.sync.dma_start(out=out_view[:, b // 4, b % 4, :], in_=block[b]["result"][:])

        first_half, second_half = slice(0, 2), slice(2, N_CHUNKS)
        last = N_BLOCKS - 1
        with tc.manual_schedule():
            flip(k_raw, kT, 0)
            flip(q_raw, qT, 0)
            first_self_score()
            self_products(1, 1)
            self_products(2, 2)
            flip(k_raw, kT, 4)
            flip(k_raw, kT, 8)
            flip(k_raw, kT, 12)
            new_z(0)
            other_scores(0, 0)
            group_weights()
            quantise_weights()
            flip_x(0)
            flip_x(2)
            other_scores(0, 1)
            quantise_x(0)
            flip_x(4)
            flip_x(6)
            mask_other(0, 0)
            other_scores(0, 2)
            quantise_x(1)
            own_mask(0)
            flip_x(8)
            flip_x(10)
            mask_other(0, 1)
            own_scores(0)
            quantise_x(2)
            flip_x(12)
            flip_x(14)
            mask_other(0, 2)
            move_own(0)
            own_mask(1)
            values(0)
            quantise_x(3)
            for b in range(N_BLOCKS + 1):
                if b in (0, 2):
                    load_q(2 * b + 8)
                if b + AHEAD < N_BLOCKS:
                    load_adjacency(b + AHEAD)
                if b < N_BLOCKS:
                    if b > 0:
                        new_z(b)
                        for k in range(OWN):
                            mask_other(b, k)
                    if b == 1 or b == 2:
                        quantise_values(2 * b - 2)
                        quantise_values(2 * b - 1)
                    if b > 0:
                        move_own(b)
                if b + 1 < N_BLOCKS:
                    other_scores(b + 1, 0)
                    other_scores(b + 1, 1)
                if b == 0:
                    other_scores(b + 1, 2)
                if b == 0:
                    values(1)
                    own_scores(1)
                    values(2)
                    values(3)
                if 1 <= b < N_BLOCKS:
                    exponentials(b - 1, first_half, 0)
                    exponentials(b - 1, second_half, 1)
                    transposes(b - 1, first_half)
                    if b < last:
                        other_scores(b + 1, 2)
                    transposes(b - 1, second_half)
                    add_sums(b - 1)
                if 1 <= b < last:
                    own_mask(b + 1)
                if b == 0:
                    self_scores(1, 3)
                if 3 <= b < N_BLOCKS:
                    finish(b - 3)
                if b == N_BLOCKS - AHEAD:
                    for done in range(b - 2):
                        store(done)
                if N_BLOCKS - AHEAD < b < N_BLOCKS:
                    store(b - 3)
                if 1 <= b < N_BLOCKS:
                    regroup(b - 1, first_half)
                    regroup(b - 1, second_half)
                if 1 <= b < 7:
                    self_products(2 * b + 2, 2)
                if b in (2, 5, 8):
                    flip_copy(q_flipped, qT, 4 * (b // 3) + 4)
                if 3 <= b < 9:
                    self_scores(2 * b - 2, 2)
                if b >= 2:
                    quantise(b - 2, slice(0, N_PASSES))
                    invert(b - 2, 1)
                if 2 <= b < N_BLOCKS:
                    weighted_sum(b - 2)
                if 0 < b < last:
                    own_scores(b + 1)
                if b in (1, 4, 7):
                    q_flipped = flip_transposes(q_raw, qT, 4 * (b // 3) + 4)
                if b < N_BLOCKS:
                    minimum(b)
            exponentials(last, first_half, 0)
            exponentials(last, slice(2, 3), 1)
            exponentials(last, slice(3, 4), 2)
            transposes(last, first_half)
            transposes(last, slice(2, 3), psum_s, "s")
            transposes(last, slice(3, 4), psum_s, "s")
            finish(last - 2)
            store(last - 2)
            regroup(last, first_half, nc.vector.tensor_copy)
            regroup(last, slice(2, 3), nc.vector.tensor_copy)
            quantise(last, first_half)
            weighted_sum(last - 1)
            regroup(last, slice(3, 4))
            quantise(last, slice(2, 3))
            finish(last - 1)
            store(last - 1)
            invert(last, 3)
            quantise(last, slice(3, 4))
            weighted_sum(last)
            finish(last)
            store(last)
